import numpy as np
import ml_dtypes


def mxq(x, axis, fmt="e4m3"):
    dtype, down = {"e4m3": (ml_dtypes.float8_e4m3fn, 7), "e5m2": (ml_dtypes.float8_e5m2, 14)}[fmt]
    v = np.moveaxis(np.asarray(x, np.float32).astype(ml_dtypes.bfloat16).astype(np.float64), axis, -1)
    blocks = v.reshape(v.shape[:-1] + (-1, 32))
    amax = np.abs(blocks).max(-1, keepdims=True)
    byte = np.maximum(np.where(amax > 0, np.frexp(amax)[1] - 1 + 127, 0) - down, 1)
    scale = np.exp2(byte - 127.0)
    codes = (blocks / scale).astype(np.float32).astype(dtype).astype(np.float64)
    return np.moveaxis((codes * scale).reshape(v.shape), -1, axis)


WIDE = False


def mx_kscale(k):
    if not WIDE:
        return np.ones(k)
    levels = np.array([10, -10, 5, -5, 0])
    a = np.random.permutation(np.resize(levels, k // 512 * 4)).reshape(k // 512, 4)
    idx = np.arange(k)
    return np.exp2(a[idx // 512, idx % 128 // 32])


BF16 = ml_dtypes.bfloat16


def bf(x):
    return np.asarray(x, np.float32).astype(BF16)


def f64(x):
    return np.asarray(x).astype(np.float64)


U1, U2, BATCH = 256, 256, 4096
K = (U1 + U2) * 3
N = U2 * 3
PROBS = [[1.0, 0.5, 0.0, 1.0, 0.5, 0.0], [0.5, 0.75, 0.5, 0.5, 0.75, 0.5], [0.0, 0.5, 1.0, 0.0, 0.5, 1.0]]


def build_mask():
    edges = [0, U1, 2 * U1, 3 * U1, 3 * U1 + U2, 3 * U1 + 2 * U2, 3 * U1 + 3 * U2]
    p = np.zeros((N, K))
    for ub in range(len(PROBS)):
        for j in range(len(PROBS[ub])):
            p[ub * U2:(ub + 1) * U2, edges[j]:edges[j + 1]] = PROBS[ub][j]
    return (np.random.random((N, K)) < p).astype(np.float64)


def setup_inputs():
    s = mx_kscale(K)
    return {"x": bf(np.random.standard_normal((BATCH, K)) * s),
            "w": bf(np.random.uniform(0.0, 2.5 / np.sqrt(K), (K, N)) / s[:, None]),
            "b": bf(np.random.standard_normal(N) * 0.3),
            "mask": bf(build_mask())}


def reference(x, w, b, mask):
    wm = f64(mask).T * f64(w)
    return (mxq(f64(x), 1, "e4m3") @ mxq(wm, 0, "e4m3")) + f64(b)

@@ -1,0 +1,273 @@
+from contextlib import ExitStack
+
+import concourse.mybir as mybir
+from concourse.masks import make_identity
+
+F32 = mybir.dt.float32
+BF16 = mybir.dt.bfloat16
+U32 = mybir.dt.uint32
+U8 = mybir.dt.uint8
+FP8X4 = mybir.dt.float8_e4m3fn_x4
+ADD = mybir.AluOpType.add
+MULT = mybir.AluOpType.mult
+
+ROWS, K, N = 4096, 1536, 768
+P = 128
+HB = 64
+SLOTS = 13
+ROW_W = SLOTS * HB
+CHUNKS = (2, 2, 4, 4, 4, 4, 4, 4, 2, 2)
+MOVES = ((4, 12), (10, 4), (2, 10), (8, 2), (0, 8), (6, 0))
+REGIONS = ((1, 0), (1, 2), (1, 1), (0, 0), (0, 1), (2, 1), (2, 2))
+ONES = ((0, 0), (2, 2))
+COLS = ((0, 512), (0, 768), (256, 768))
+OPS_OF_UB = ((0, 1), (0, 1, 2), (1, 2))
+
+FLOPS = 2 * ROWS * K * N
+BYTES = ROWS * K * 2 + ROWS * N * 4 + 14 * 131072 + 10 * 131072 + N * 2
+
+
+def tile_gpi_t_kernel(tc, x, w, b, mask, out):
+    nc = tc.nc
+    with ExitStack() as ctx:
+        const = ctx.enter_context(tc.tile_pool(name="const", bufs=1))
+        wpool = ctx.enter_context(tc.tile_pool(name="wpool", bufs=1))
+        wgpool = ctx.enter_context(tc.tile_pool(name="wgpool", bufs=3))
+        xpool = ctx.enter_context(tc.tile_pool(name="xpool", bufs=7))
+        gpool = ctx.enter_context(tc.tile_pool(name="gpool", bufs=6))
+        cpool = ctx.enter_context(tc.tile_pool(name="cpool", bufs=9))
+        opool = ctx.enter_context(tc.tile_pool(name="opool", bufs=3))
+        ps_t = ctx.enter_context(tc.psum_pool(name="ps_t", bufs=3))
+        ps_o = ctx.enter_context(tc.psum_pool(name="ps_o", bufs=5))
+
+        ident = const.tile([P, P], F32, name="ident")
+        make_identity(nc, ident[:])
+        ones = const.tile([P, P], BF16, name="ones")
+        nc.vector.memset(ones[:], 1.0)
+        brow = const.tile([P, N], BF16, name="brow")
+        nc.vector.memset(brow[:], 0.0)
+        nc.scalar.dma_start(out=brow[0:1, :], in_=b.rearrange("(o n) -> o n", o=1))
+
+        m_blocks = mask.rearrange("(b j e) k -> b j (e k)", b=3, j=P, e=2).rearrange(
+            "b j (i k) -> b j i k", k=256
+        )
+        w_v = w.rearrange("(s o u p) n -> s o p u n", s=2, o=3, u=2, p=P)
+        mask_sb = {}
+        wt = {}
+
+        def load_mask(ub):
+            if ub == 1:
+                m_t = wpool.tile([P, 2 * K], BF16, name="m1")
+                nc.sync.dma_start(
+                    out=m_t[:].rearrange("p (i k) -> p i k", k=256), in_=m_blocks[1]
+                )
+            else:
+                m_t = wpool.tile([P, 4 * 256], BF16, name="m%d" % ub)
+                nc.sync.dma_start(
+                    out=m_t[:].rearrange("p (i k) -> p i k", k=256),
+                    in_=m_blocks[ub][:, 1:12:3, :],
+                )
+            mask_sb[ub] = m_t
+
+        def load_w(s, o):
+            c0, c1 = COLS[o]
+            w_t = wpool.tile([P, 2 * (c1 - c0)], BF16, name="w%d%d" % (s, o))
+            nc.sync.dma_start(
+                out=w_t[:].rearrange("p (u n) -> p u n", u=2), in_=w_v[s, o][:, :, c0:c1]
+            )
+            wt[(s, o)] = w_t
+
+        chunk_rows = []
+        r0 = 0
+        for jn in CHUNKS:
+            chunk_rows.append(r0)
+            r0 += P * jn
+        xw = {}
+
+        def load_x(ci):
+            jn = CHUNKS[ci]
+            x_t = xpool.tile([P, jn * ROW_W * 2], BF16, tag="x", name="x%d" % ci)
+            ra = chunk_rows[ci]
+            nc.sync.dma_start(
+                out=x_t[:].rearrange("p (j c) -> p j c", j=jn)[:, :, 0:K],
+                in_=x[ra : ra + P * jn, :].rearrange("(p j) k -> p j k", j=jn),
+            )
+            xw[ci] = x_t[:].bitcast(F32)
+
+        def move_x(ci):
+            xs = xw[ci].rearrange("p (j s c) -> p j s c", j=CHUNKS[ci], s=SLOTS)
+            for src, dst in MOVES:
+                nc.scalar.copy(out=xs[:, :, dst, :], in_=xs[:, :, src, :])
+
+        load_mask(0)
+        load_w(0, 1)
+        load_w(1, 1)
+        load_mask(2)
+        load_mask(1)
+        load_w(0, 0)
+        load_w(1, 0)
+        load_x(0)
+        load_w(0, 2)
+        load_w(1, 2)
+        for ci in range(1, 7):
+            load_x(ci)
+
+        pb_a = ps_o.tile([P, 512], F32, tag="O", name="pb_a")
+        nc.tensor.matmul(out=pb_a[:], lhsT=ones[:], rhs=brow[:, 0:512], start=True, stop=True)
+        bias_a = const.tile([P, 512], F32, name="bias_a")
+        nc.vector.tensor_copy(out=bias_a[:], in_=pb_a[:])
+        pb_b = ps_o.tile([P, 512], F32, tag="O", name="pb_b")
+        for t in range(2):
+            nc.tensor.matmul(
+                out=pb_b[:, 256 * t : 256 * t + 256],
+                lhsT=ones[:],
+                rhs=brow[:, 512:768],
+                start=True,
+                stop=True,
+            )
+        bias_b = const.tile([P, 512], F32, name="bias_b")
+        nc.vector.tensor_copy(out=bias_b[:], in_=pb_b[:])
+
+        wc = wpool.tile([P, 7 * 256], U32, name="wc", align_bytes=64)
+        wsc = wpool.tile([P, 7 * 256], U8, name="wsc", align_bytes=64)
+
+        def t1(bank, slot, s, o, u, ub):
+            c0, c1 = COLS[o]
+            off = (u * (c1 - c0) + ub * 256 - c0) // 2
+            nc.tensor.transpose(
+                bank[:, slot * P : (slot + 1) * P],
+                wt[(s, o)][:].bitcast(F32)[:, off : off + P],
+                ident[:],
+            )
+
+        def prep_region(r):
+            o, ub = REGIONS[r]
+            bank = ps_o.tile([P, 512], F32, tag="O", name="t1_%d" % r)
+            wtr = wpool.tile([P, 1024], BF16, name="wtr%d" % r)
+            if (o, ub) in ONES:
+                for slot, (s, u) in enumerate(((1, 0), (0, 1), (1, 1), (0, 0))):
+                    t1(bank, slot, s, o, u, ub)
+                nc.scalar.copy(
+                    out=wtr[:].rearrange("p (e m) -> p e m", e=2),
+                    in_=bank[:].bitcast(BF16).rearrange("p (m e) -> p e m", e=2),
+                )
+            else:
+                for slot, (s, u) in enumerate(((1, 0), (1, 1), (0, 1), (0, 0))):
+                    t1(bank, slot, s, o, u, ub)
+                bv = bank[:].bitcast(BF16).rearrange("p (l k e) -> p e l k", l=4, e=2)
+                wv = wtr[:].rearrange("p (e l k) -> p e l k", e=2, l=4)
+                mv = mask_sb[ub][:].rearrange("p (e h k) -> p e h k", e=2, k=P)
+                f0 = 2 * o if ub == 1 else 0
+                s0 = 6 + 2 * o if ub == 1 else 2
+                nc.vector.tensor_tensor(
+                    out=wv[:, :, 0:4:2, :], in0=bv[:, :, 0:2, :], in1=mv[:, :, s0 : s0 + 2, :], op=MULT
+                )
+                nc.vector.tensor_tensor(
+                    out=wv[:, :, 1, :], in0=bv[:, :, 2, :], in1=mv[:, :, f0 + 1, :], op=MULT
+                )
+                nc.vector.tensor_tensor(
+                    out=wv[:, :, 3, :], in0=bv[:, :, 3, :], in1=mv[:, :, f0, :], op=MULT
+                )
+            bank2 = ps_o.tile([P, 512], F32, tag="O", name="t2_%d" % r)
+            wf = wtr[:].bitcast(F32)
+            for i in range(4):
+                nc.tensor.transpose(bank2[:, i * P : (i + 1) * P], wf[:, i * P : (i + 1) * P], ident[:])
+            wg = wgpool.tile([P, 1024], BF16, tag="wg", name="wg%d" % r, align_bytes=64)
+            nc.scalar.copy(
+                out=wg[:].bitcast(F32).rearrange("p (j e u) -> p j e u", e=2, u=2),
+                in_=bank2[:].rearrange("p (e u j) -> p j e u", e=2, u=2),
+            )
+            nc.vector.quantize_mx(
+                out=wc[:, r * 256 : (r + 1) * 256].bitcast(FP8X4),
+                scales=wsc[:, r * 256 : (r + 1) * 256],
+                in_=wg[:],
+            )
+
+        for r in range(len(REGIONS)):
+            prep_region(r)
+
+        pairs = []
+        for ci, jn in enumerate(CHUNKS):
+            for j0 in range(0, jn, 2):
+                pairs.append((ci, j0))
+        codes = {}
+        ost = {}
+
+        def stage_t(n):
+            ci, j0 = pairs[n]
+            if j0 == 0:
+                move_x(ci)
+            got = []
+            for bk in range(3):
+                pt = ps_t.tile([P, 512], F32, tag="T", name="pt%d_%d" % (n, bk))
+                for sl in range(2):
+                    t, o = divmod(2 * bk + sl, 3)
+                    for u in range(2):
+                        off = (j0 + t) * ROW_W + HB * (2 * o + 7 * u)
+                        i = 2 * sl + u
+                        nc.tensor.transpose(
+                            pt[:, i * P : (i + 1) * P], xw[ci][:, off : off + P], ident[:]
+                        )
+                grp = gpool.tile([P, 1024], BF16, tag="g", name="g%d_%d" % (n, bk), align_bytes=64)
+                nc.scalar.copy(
+                    out=grp[:].bitcast(F32).rearrange("p (s r u) -> p s r u", s=2, u=2),
+                    in_=pt[:].rearrange("p (s u r) -> p s r u", s=2, u=2),
+                )
+                cod = cpool.tile([P, 256], U32, tag="c", name="c%d_%d" % (n, bk), align_bytes=64)
+                scl = cpool.tile([P, 256], U8, tag="s", name="s%d_%d" % (n, bk), align_bytes=64)
+                nc.vector.quantize_mx(out=cod[:].bitcast(FP8X4), scales=scl[:], in_=grp[:])
+                got.append((cod, scl))
+            codes[n] = got
+
+        def group(n, acc, t, ub):
+            ops = OPS_OF_UB[ub]
+            for o in ops:
+                bk, sl = divmod(3 * t + o, 2)
+                cod, scl = codes[n][bk]
+                r = REGIONS.index((o, ub))
+                nc.tensor.matmul_mx(
+                    out=acc,
+                    lhsT=cod[:, sl * P : (sl + 1) * P].bitcast(FP8X4),
+                    lhsT_scale=scl[:, sl * P : (sl + 1) * P],
+                    rhs=wc[:, r * 256 : (r + 1) * 256].bitcast(FP8X4),
+                    rhs_scale=wsc[:, r * 256 : (r + 1) * 256],
+                    start=(o == ops[0]),
+                    stop=(o == ops[-1]),
+                )
+
+        def stage_mx(n):
+            ci, j0 = pairs[n]
+            jn = CHUNKS[ci]
+            if j0 == 0:
+                ost[ci] = opool.tile([P, jn * N], F32, tag="o", name="o%d" % ci)
+            ov = ost[ci][:].rearrange("p (j n) -> p j n", n=N)
+            for t in range(2):
+                acc = ps_o.tile([P, 512], F32, tag="O", name="acc%d_%d" % (n, t))
+                group(n, acc[:, 0:256], t, 0)
+                group(n, acc[:, 256:512], t, 1)
+                nc.vector.tensor_tensor(out=ov[:, j0 + t, 0:512], in0=acc[:], in1=bias_a[:], op=ADD)
+            acy = ps_o.tile([P, 512], F32, tag="O", name="acy%d" % n)
+            for t in range(2):
+                group(n, acy[:, 256 * t : 256 * t + 256], t, 2)
+            nc.vector.tensor_tensor(
+                out=ov[:, j0 : j0 + 2, 512:768],
+                in0=acy[:].rearrange("p (t n) -> p t n", t=2),
+                in1=bias_b[:].rearrange("p (t n) -> p t n", t=2),
+                op=ADD,
+            )
+            if j0 + 2 == jn:
+                ra = chunk_rows[ci]
+                nc.sync.dma_start(
+                    out=out[ra : ra + P * jn, :].rearrange("(p j) n -> p (j n)", j=jn),
+                    in_=ost[ci][:],
+                )
+                if ci + 7 < len(CHUNKS):
+                    load_x(ci + 7)
+
+        np_ = len(pairs)
+        stage_t(0)
+        stage_t(1)
+        for n in range(np_):
+            if n + 2 < np_:
+                stage_t(n + 2)
+            stage_mx(n)

@@ -16,10 +16,10 @@ P = 128
 HB = 64
 SLOTS = 13
 ROW_W = SLOTS * HB
-CHUNKS = (2, 2, 4, 4, 4, 4, 4, 4, 2, 2)
+CHUNKS = (2, 2, 2, 2, 4, 4, 4, 4, 4, 2, 2)
+RING = 7
 MOVES = ((4, 12), (10, 4), (2, 10), (8, 2), (0, 8), (6, 0))
 REGIONS = ((1, 0), (1, 2), (1, 1), (0, 0), (0, 1), (2, 1), (2, 2))
-ONES = ((0, 0), (2, 2))
 COLS = ((0, 512), (0, 768), (256, 768))
 OPS_OF_UB = ((0, 1), (0, 1, 2), (1, 2))
 
@@ -32,13 +32,13 @@ def tile_gpi_t_kernel(tc, x, w, b, mask, out):
     with ExitStack() as ctx:
         const = ctx.enter_context(tc.tile_pool(name="const", bufs=1))
         wpool = ctx.enter_context(tc.tile_pool(name="wpool", bufs=1))
-        wgpool = ctx.enter_context(tc.tile_pool(name="wgpool", bufs=3))
-        xpool = ctx.enter_context(tc.tile_pool(name="xpool", bufs=7))
+        xpool = ctx.enter_context(tc.tile_pool(name="xpool", bufs=RING))
         gpool = ctx.enter_context(tc.tile_pool(name="gpool", bufs=6))
         cpool = ctx.enter_context(tc.tile_pool(name="cpool", bufs=9))
         opool = ctx.enter_context(tc.tile_pool(name="opool", bufs=3))
         ps_t = ctx.enter_context(tc.psum_pool(name="ps_t", bufs=3))
         ps_o = ctx.enter_context(tc.psum_pool(name="ps_o", bufs=5))
+        ctx.enter_context(tc.manual_schedule())
 
         ident = const.tile([P, P], F32, name="ident")
         make_identity(nc, ident[:])
@@ -78,10 +78,16 @@ def tile_gpi_t_kernel(tc, x, w, b, mask, out):
             wt[(s, o)] = w_t
 
         chunk_rows = []
+        first_pair = []
+        pairs = []
         r0 = 0
-        for jn in CHUNKS:
+        for ci, jn in enumerate(CHUNKS):
             chunk_rows.append(r0)
+            first_pair.append(len(pairs))
             r0 += P * jn
+            for j0 in range(0, jn, 2):
+                pairs.append((ci, j0))
+        n_pairs = len(pairs)
         xw = {}
 
         def load_x(ci):
@@ -94,28 +100,28 @@ def tile_gpi_t_kernel(tc, x, w, b, mask, out):
             )
             xw[ci] = x_t[:].bitcast(F32)
 
-        def move_x(ci):
+        def move_x(ci, lo, hi):
             xs = xw[ci].rearrange("p (j s c) -> p j s c", j=CHUNKS[ci], s=SLOTS)
-            for src, dst in MOVES:
+            for src, dst in MOVES[lo:hi]:
                 nc.scalar.copy(out=xs[:, :, dst, :], in_=xs[:, :, src, :])
 
         load_mask(0)
         load_w(0, 1)
         load_w(1, 1)
+        load_x(0)
         load_mask(2)
         load_mask(1)
         load_w(0, 0)
         load_w(1, 0)
-        load_x(0)
         load_w(0, 2)
         load_w(1, 2)
-        for ci in range(1, 7):
+        for ci in range(1, RING):
             load_x(ci)
 
         pb_a = ps_o.tile([P, 512], F32, tag="O", name="pb_a")
         nc.tensor.matmul(out=pb_a[:], lhsT=ones[:], rhs=brow[:, 0:512], start=True, stop=True)
         bias_a = const.tile([P, 512], F32, name="bias_a")
-        nc.vector.tensor_copy(out=bias_a[:], in_=pb_a[:])
+        nc.scalar.copy(out=bias_a[:], in_=pb_a[:])
         pb_b = ps_o.tile([P, 512], F32, tag="O", name="pb_b")
         for t in range(2):
             nc.tensor.matmul(
@@ -126,78 +132,89 @@ def tile_gpi_t_kernel(tc, x, w, b, mask, out):
                 stop=True,
             )
         bias_b = const.tile([P, 512], F32, name="bias_b")
-        nc.vector.tensor_copy(out=bias_b[:], in_=pb_b[:])
+        nc.scalar.copy(out=bias_b[:], in_=pb_b[:])
 
         wc = wpool.tile([P, 7 * 256], U32, name="wc", align_bytes=64)
         wsc = wpool.tile([P, 7 * 256], U8, name="wsc", align_bytes=64)
+        bank1 = {}
+        bank2 = {}
+        wtr = {}
+        wgr = {}
+        ORDER = ((1, 0), (0, 1), (1, 1), (0, 0))
 
-        def t1(bank, slot, s, o, u, ub):
+        def t1(reg, s):
+            o, ub = reg
+            if reg not in bank1:
+                bank1[reg] = ps_o.tile([P, 512], F32, tag="O", name="t1_%d%d" % reg)
+                wtr[reg] = wpool.tile([P, 1024], BF16, name="wtr%d%d" % reg)
             c0, c1 = COLS[o]
-            off = (u * (c1 - c0) + ub * 256 - c0) // 2
-            nc.tensor.transpose(
-                bank[:, slot * P : (slot + 1) * P],
-                wt[(s, o)][:].bitcast(F32)[:, off : off + P],
-                ident[:],
-            )
+            for slot, (s_, u) in enumerate(ORDER):
+                if s_ == s:
+                    off = (u * (c1 - c0) + ub * 256 - c0) // 2
+                    nc.tensor.transpose(
+                        bank1[reg][:, slot * P : (slot + 1) * P],
+                        wt[(s, o)][:].bitcast(F32)[:, off : off + P],
+                        ident[:],
+                    )
 
-        def prep_region(r):
-            o, ub = REGIONS[r]
-            bank = ps_o.tile([P, 512], F32, tag="O", name="t1_%d" % r)
-            wtr = wpool.tile([P, 1024], BF16, name="wtr%d" % r)
-            if (o, ub) in ONES:
-                for slot, (s, u) in enumerate(((1, 0), (0, 1), (1, 1), (0, 0))):
-                    t1(bank, slot, s, o, u, ub)
-                nc.scalar.copy(
-                    out=wtr[:].rearrange("p (e m) -> p e m", e=2),
-                    in_=bank[:].bitcast(BF16).rearrange("p (m e) -> p e m", e=2),
+        def views(reg):
+            bv = bank1[reg][:].bitcast(BF16).rearrange("p (l k e) -> p e l k", l=4, e=2)
+            wv = wtr[reg][:].rearrange("p (e l k) -> p e l k", e=2, l=4)
+            return bv, wv
+
+        def ones_copy(reg, s):
+            bv, wv = views(reg)
+            lo = 0 if s == 1 else 1
+            nc.scalar.copy(out=wv[:, :, lo:4:2, :], in_=bv[:, :, lo:4:2, :])
+
+        def mult(reg, s):
+            o, ub = reg
+            bv, wv = views(reg)
+            mv = mask_sb[ub][:].rearrange("p (e h k) -> p e h k", e=2, k=P)
+            f0 = 2 * o if ub == 1 else 0
+            s0 = 6 + 2 * o if ub == 1 else 2
+            if s == 1:
+                nc.vector.tensor_tensor(
+                    out=wv[:, :, 0:4:2, :], in0=bv[:, :, 0:4:2, :], in1=mv[:, :, s0 : s0 + 2, :], op=MULT
                 )
             else:
-                for slot, (s, u) in enumerate(((1, 0), (1, 1), (0, 1), (0, 0))):
-                    t1(bank, slot, s, o, u, ub)
-                bv = bank[:].bitcast(BF16).rearrange("p (l k e) -> p e l k", l=4, e=2)
-                wv = wtr[:].rearrange("p (e l k) -> p e l k", e=2, l=4)
-                mv = mask_sb[ub][:].rearrange("p (e h k) -> p e h k", e=2, k=P)
-                f0 = 2 * o if ub == 1 else 0
-                s0 = 6 + 2 * o if ub == 1 else 2
                 nc.vector.tensor_tensor(
-                    out=wv[:, :, 0:4:2, :], in0=bv[:, :, 0:2, :], in1=mv[:, :, s0 : s0 + 2, :], op=MULT
-                )
-                nc.vector.tensor_tensor(
-                    out=wv[:, :, 1, :], in0=bv[:, :, 2, :], in1=mv[:, :, f0 + 1, :], op=MULT
+                    out=wv[:, :, 1, :], in0=bv[:, :, 1, :], in1=mv[:, :, f0 + 1, :], op=MULT
                 )
                 nc.vector.tensor_tensor(
                     out=wv[:, :, 3, :], in0=bv[:, :, 3, :], in1=mv[:, :, f0, :], op=MULT
                 )
-            bank2 = ps_o.tile([P, 512], F32, tag="O", name="t2_%d" % r)
-            wf = wtr[:].bitcast(F32)
+
+        def t2(reg, pool, tag):
+            bank2[reg] = pool.tile([P, 512], F32, tag=tag, name="t2_%d%d" % reg)
+            wf = wtr[reg][:].bitcast(F32)
             for i in range(4):
-                nc.tensor.transpose(bank2[:, i * P : (i + 1) * P], wf[:, i * P : (i + 1) * P], ident[:])
-            wg = wgpool.tile([P, 1024], BF16, tag="wg", name="wg%d" % r, align_bytes=64)
+                nc.tensor.transpose(
+                    bank2[reg][:, i * P : (i + 1) * P], wf[:, i * P : (i + 1) * P], ident[:]
+                )
+
+        def x2(reg):
+            wgr[reg] = wpool.tile([P, 1024], BF16, name="wg%d%d" % reg, align_bytes=64)
             nc.scalar.copy(
-                out=wg[:].bitcast(F32).rearrange("p (j e u) -> p j e u", e=2, u=2),
-                in_=bank2[:].rearrange("p (e u j) -> p j e u", e=2, u=2),
+                out=wgr[reg][:].bitcast(F32).rearrange("p (j e u) -> p j e u", e=2, u=2),
+                in_=bank2[reg][:].rearrange("p (e u j) -> p j e u", e=2, u=2),
             )
+
+        def wq(reg):
+            r = REGIONS.index(reg)
             nc.vector.quantize_mx(
                 out=wc[:, r * 256 : (r + 1) * 256].bitcast(FP8X4),
                 scales=wsc[:, r * 256 : (r + 1) * 256],
-                in_=wg[:],
+                in_=wgr[reg][:],
             )
 
-        for r in range(len(REGIONS)):
-            prep_region(r)
-
-        pairs = []
-        for ci, jn in enumerate(CHUNKS):
-            for j0 in range(0, jn, 2):
-                pairs.append((ci, j0))
+        grouped = {}
         codes = {}
         ost = {}
+        acc = {}
 
         def stage_t(n):
             ci, j0 = pairs[n]
-            if j0 == 0:
-                move_x(ci)
-            got = []
             for bk in range(3):
                 pt = ps_t.tile([P, 512], F32, tag="T", name="pt%d_%d" % (n, bk))
                 for sl in range(2):
@@ -213,61 +230,155 @@ def tile_gpi_t_kernel(tc, x, w, b, mask, out):
                     out=grp[:].bitcast(F32).rearrange("p (s r u) -> p s r u", s=2, u=2),
                     in_=pt[:].rearrange("p (s u r) -> p s r u", s=2, u=2),
                 )
-                cod = cpool.tile([P, 256], U32, tag="c", name="c%d_%d" % (n, bk), align_bytes=64)
-                scl = cpool.tile([P, 256], U8, tag="s", name="s%d_%d" % (n, bk), align_bytes=64)
-                nc.vector.quantize_mx(out=cod[:].bitcast(FP8X4), scales=scl[:], in_=grp[:])
-                got.append((cod, scl))
-            codes[n] = got
+                grouped[(n, bk)] = grp
+            if j0 + 2 == CHUNKS[ci] and ci + RING < len(CHUNKS):
+                load_x(ci + RING)
 
-        def group(n, acc, t, ub):
+        def fill_moves(m):
+            for ci, jn in enumerate(CHUNKS):
+                if jn == 2 and first_pair[ci] == m + 1:
+                    move_x(ci, 0, 6)
+                if jn == 4 and first_pair[ci] == m + 2:
+                    move_x(ci, 0, 3)
+                if jn == 4 and first_pair[ci] == m + 1:
+                    move_x(ci, 3, 6)
+
+        def quant(n, bk):
+            cod = cpool.tile([P, 256], U32, tag="c", name="c%d_%d" % (n, bk), align_bytes=64)
+            scl = cpool.tile([P, 256], U8, tag="s", name="s%d_%d" % (n, bk), align_bytes=64)
+            nc.vector.quantize_mx(out=cod[:].bitcast(FP8X4), scales=scl[:], in_=grouped[(n, bk)][:])
+            codes[(n, bk)] = (cod, scl)
+
+        def one_pass(n, t, ub, o):
             ops = OPS_OF_UB[ub]
-            for o in ops:
-                bk, sl = divmod(3 * t + o, 2)
-                cod, scl = codes[n][bk]
-                r = REGIONS.index((o, ub))
-                nc.tensor.matmul_mx(
-                    out=acc,
-                    lhsT=cod[:, sl * P : (sl + 1) * P].bitcast(FP8X4),
-                    lhsT_scale=scl[:, sl * P : (sl + 1) * P],
-                    rhs=wc[:, r * 256 : (r + 1) * 256].bitcast(FP8X4),
-                    rhs_scale=wsc[:, r * 256 : (r + 1) * 256],
-                    start=(o == ops[0]),
-                    stop=(o == ops[-1]),
-                )
+            bk, sl = divmod(3 * t + o, 2)
+            cod, scl = codes[(n, bk)]
+            r = REGIONS.index((o, ub))
+            if ub == 2:
+                dst = acc[(n, 2)][:, 256 * t : 256 * t + 256]
+            else:
+                dst = acc[(n, t)][:, 256 * ub : 256 * ub + 256]
+            nc.tensor.matmul_mx(
+                out=dst,
+                lhsT=cod[:, sl * P : (sl + 1) * P].bitcast(FP8X4),
+                lhsT_scale=scl[:, sl * P : (sl + 1) * P],
+                rhs=wc[:, r * 256 : (r + 1) * 256].bitcast(FP8X4),
+                rhs_scale=wsc[:, r * 256 : (r + 1) * 256],
+                start=(o == ops[0]),
+                stop=(o == ops[-1]),
+            )
 
-        def stage_mx(n):
+        def stage_mx(n, late_c):
+            for i in range(3):
+                acc[(n, i)] = ps_o.tile([P, 512], F32, tag="O", name="acc%d_%d" % (n, i))
+            if late_c:
+                order = [(0, 0, 0), (0, 0, 1), (0, 1, 0), (0, 1, 1), (1, 0, 0), (1, 0, 1), (1, 1, 0), (1, 1, 1)]
+                order += [(0, 2, 1), (0, 1, 2), (1, 1, 2), (0, 2, 2), (1, 2, 1), (1, 2, 2)]
+            else:
+                order = [(t, ub, o) for t in range(2) for ub in range(2) for o in OPS_OF_UB[ub]]
+                order += [(t, 2, o) for t in range(2) for o in OPS_OF_UB[2]]
+            for t, ub, o in order:
+                one_pass(n, t, ub, o)
+
+        def evac(n, i):
             ci, j0 = pairs[n]
             jn = CHUNKS[ci]
-            if j0 == 0:
+            if j0 == 0 and i == 0:
                 ost[ci] = opool.tile([P, jn * N], F32, tag="o", name="o%d" % ci)
             ov = ost[ci][:].rearrange("p (j n) -> p j n", n=N)
-            for t in range(2):
-                acc = ps_o.tile([P, 512], F32, tag="O", name="acc%d_%d" % (n, t))
-                group(n, acc[:, 0:256], t, 0)
-                group(n, acc[:, 256:512], t, 1)
-                nc.vector.tensor_tensor(out=ov[:, j0 + t, 0:512], in0=acc[:], in1=bias_a[:], op=ADD)
-            acy = ps_o.tile([P, 512], F32, tag="O", name="acy%d" % n)
-            for t in range(2):
-                group(n, acy[:, 256 * t : 256 * t + 256], t, 2)
-            nc.vector.tensor_tensor(
-                out=ov[:, j0 : j0 + 2, 512:768],
-                in0=acy[:].rearrange("p (t n) -> p t n", t=2),
-                in1=bias_b[:].rearrange("p (t n) -> p t n", t=2),
-                op=ADD,
-            )
-            if j0 + 2 == jn:
-                ra = chunk_rows[ci]
-                nc.sync.dma_start(
-                    out=out[ra : ra + P * jn, :].rearrange("(p j) n -> p (j n)", j=jn),
-                    in_=ost[ci][:],
+            if i < 2:
+                nc.vector.tensor_tensor(
+                    out=ov[:, j0 + i, 0:512], in0=acc[(n, i)][:], in1=bias_a[:], op=ADD
                 )
-                if ci + 7 < len(CHUNKS):
-                    load_x(ci + 7)
+            else:
+                nc.vector.tensor_tensor(
+                    out=ov[:, j0 : j0 + 2, 512:768],
+                    in0=acc[(n, 2)][:].rearrange("p (t n) -> p t n", t=2),
+                    in1=bias_b[:].rearrange("p (t n) -> p t n", t=2),
+                    op=ADD,
+                )
+                if j0 + 2 == jn:
+                    ra = chunk_rows[ci]
+                    nc.gpsimd.dma_start(
+                        out=out[ra : ra + P * jn, :].rearrange("(p j) n -> p (j n)", j=jn),
+                        in_=ost[ci][:],
+                    )
 
-        np_ = len(pairs)
+        b0, b2, b1, a0, a1, c1r, c2r = REGIONS
+        for reg in (b0, b2, b1):
+            t1(reg, 0)
+            t1(reg, 1)
+        mult(b0, 1)
+        mult(b0, 0)
+        t2(b0, ps_o, "O")
+        move_x(0, 0, 6)
+        x2(b0)
         stage_t(0)
+        mult(b2, 1)
+        mult(b2, 0)
+        wq(b0)
+        quant(0, 0)
+        t2(b2, ps_o, "O")
+        x2(b2)
+        mult(b1, 1)
+        mult(b1, 0)
+        quant(0, 1)
+        quant(0, 2)
+        wq(b2)
+        t1(a0, 0)
+        t1(a1, 0)
+        t1(a0, 1)
+        t1(a1, 1)
+        t2(b1, ps_t, "T")
+        ones_copy(a0, 0)
+        ones_copy(a0, 1)
+        x2(b1)
+        mult(a1, 0)
+        mult(a1, 1)
+        wq(b1)
+        t1(c2r, 0)
+        t1(c1r, 0)
+        t2(a0, ps_t, "T")
+        t1(c2r, 1)
+        t1(c1r, 1)
+        ones_copy(c2r, 0)
+        x2(a0)
+        ones_copy(c2r, 1)
+        mult(c1r, 0)
+        mult(c1r, 1)
+        wq(a0)
+        t2(a1, ps_t, "T")
+        x2(a1)
+        wq(a1)
+        t2(c2r, ps_t, "T")
+        x2(c2r)
+        t2(c1r, ps_t, "T")
+        x2(c1r)
+        wq(c2r)
+        wq(c1r)
+        fill_moves(0)
+
+        stage_mx(0, True)
         stage_t(1)
-        for n in range(np_):
-            if n + 2 < np_:
+        fill_moves(1)
+        stage_t(2)
+        fill_moves(2)
+        evac(0, 0)
+        quant(1, 0)
+        evac(0, 1)
+        quant(1, 1)
+        evac(0, 2)
+        quant(1, 2)
+        for n in range(1, n_pairs):
+            stage_mx(n, False)
+            if n + 2 < n_pairs:
                 stage_t(n + 2)
-            stage_mx(n)
+                fill_moves(n + 2)
+            if n + 1 < n_pairs:
+                quant(n + 1, 0)
+                quant(n + 1, 1)
+            evac(n, 0)
+            if n + 1 < n_pairs:
+                quant(n + 1, 2)
+            evac(n, 1)
+            evac(n, 2)

@@ -35,9 +35,9 @@ def tile_gpi_t_kernel(tc, x, w, b, mask, out):
         xpool = ctx.enter_context(tc.tile_pool(name="xpool", bufs=RING))
         gpool = ctx.enter_context(tc.tile_pool(name="gpool", bufs=6))
         cpool = ctx.enter_context(tc.tile_pool(name="cpool", bufs=9))
-        opool = ctx.enter_context(tc.tile_pool(name="opool", bufs=3))
-        ps_t = ctx.enter_context(tc.psum_pool(name="ps_t", bufs=3))
-        ps_o = ctx.enter_context(tc.psum_pool(name="ps_o", bufs=5))
+        opool = ctx.enter_context(tc.tile_pool(name="opool", bufs=5))
+        ps_t = ctx.enter_context(tc.psum_pool(name="ps_t", bufs=4))
+        ps_o = ctx.enter_context(tc.psum_pool(name="ps_o", bufs=4))
         ctx.enter_context(tc.manual_schedule())
 
         ident = const.tile([P, P], F32, name="ident")
@@ -46,7 +46,6 @@ def tile_gpi_t_kernel(tc, x, w, b, mask, out):
         nc.vector.memset(ones[:], 1.0)
         brow = const.tile([P, N], BF16, name="brow")
         nc.vector.memset(brow[:], 0.0)
-        nc.scalar.dma_start(out=brow[0:1, :], in_=b.rearrange("(o n) -> o n", o=1))
 
         m_blocks = mask.rearrange("(b j e) k -> b j (e k)", b=3, j=P, e=2).rearrange(
             "b j (i k) -> b j i k", k=256
@@ -107,6 +106,7 @@ def tile_gpi_t_kernel(tc, x, w, b, mask, out):
 
         load_mask(0)
         load_w(0, 1)
+        nc.sync.dma_start(out=brow[0:1, :], in_=b.rearrange("(o n) -> o n", o=1))
         load_w(1, 1)
         load_x(0)
         load_mask(2)
@@ -236,11 +236,11 @@ def tile_gpi_t_kernel(tc, x, w, b, mask, out):
 
         def fill_moves(m):
             for ci, jn in enumerate(CHUNKS):
-                if jn == 2 and first_pair[ci] == m + 1:
+                if jn == 2 and first_pair[ci] == m + 2 and ci > 2:
                     move_x(ci, 0, 6)
-                if jn == 4 and first_pair[ci] == m + 2:
+                if jn == 4 and first_pair[ci] == m + 3:
                     move_x(ci, 0, 3)
-                if jn == 4 and first_pair[ci] == m + 1:
+                if jn == 4 and first_pair[ci] == m + 2:
                     move_x(ci, 3, 6)
 
         def quant(n, bk):
@@ -283,26 +283,25 @@ def tile_gpi_t_kernel(tc, x, w, b, mask, out):
         def evac(n, i):
             ci, j0 = pairs[n]
             jn = CHUNKS[ci]
-            if j0 == 0 and i == 0:
-                ost[ci] = opool.tile([P, jn * N], F32, tag="o", name="o%d" % ci)
-            ov = ost[ci][:].rearrange("p (j n) -> p j n", n=N)
+            if i == 0:
+                ost[n] = opool.tile([P, 2 * N], F32, tag="o", name="o%d" % n)
+            ov = ost[n][:].rearrange("p (j n) -> p j n", n=N)
             if i < 2:
                 nc.vector.tensor_tensor(
-                    out=ov[:, j0 + i, 0:512], in0=acc[(n, i)][:], in1=bias_a[:], op=ADD
+                    out=ov[:, i, 0:512], in0=acc[(n, i)][:], in1=bias_a[:], op=ADD
                 )
             else:
                 nc.vector.tensor_tensor(
-                    out=ov[:, j0 : j0 + 2, 512:768],
+                    out=ov[:, :, 512:768],
                     in0=acc[(n, 2)][:].rearrange("p (t n) -> p t n", t=2),
                     in1=bias_b[:].rearrange("p (t n) -> p t n", t=2),
                     op=ADD,
                 )
-                if j0 + 2 == jn:
-                    ra = chunk_rows[ci]
-                    nc.gpsimd.dma_start(
-                        out=out[ra : ra + P * jn, :].rearrange("(p j) n -> p (j n)", j=jn),
-                        in_=ost[ci][:],
-                    )
+                ra = chunk_rows[ci]
+                nc.sync.dma_start(
+                    out=out[ra : ra + P * jn, :].rearrange("(p j) n -> p j n", j=jn)[:, j0 : j0 + 2, :],
+                    in_=ov,
+                )
 
         b0, b2, b1, a0, a1, c1r, c2r = REGIONS
         for reg in (b0, b2, b1):
@@ -310,7 +309,7 @@ def tile_gpi_t_kernel(tc, x, w, b, mask, out):
             t1(reg, 1)
         mult(b0, 1)
         mult(b0, 0)
-        t2(b0, ps_o, "O")
+        t2(b0, ps_t, "T")
         move_x(0, 0, 6)
         x2(b0)
         stage_t(0)
@@ -318,7 +317,7 @@ def tile_gpi_t_kernel(tc, x, w, b, mask, out):
         mult(b2, 0)
         wq(b0)
         quant(0, 0)
-        t2(b2, ps_o, "O")
+        t2(b2, ps_t, "T")
         x2(b2)
         mult(b1, 1)
         mult(b1, 0)
@@ -356,12 +355,13 @@ def tile_gpi_t_kernel(tc, x, w, b, mask, out):
         x2(c1r)
         wq(c2r)
         wq(c1r)
-        fill_moves(0)
+        move_x(1, 0, 6)
+        move_x(2, 0, 6)
 
         stage_mx(0, True)
         stage_t(1)
-        fill_moves(1)
         stage_t(2)
+        fill_moves(1)
         fill_moves(2)
         evac(0, 0)
         quant(1, 0)

@@ -16,7 +16,7 @@ P = 128
 HB = 64
 SLOTS = 13
 ROW_W = SLOTS * HB
-CHUNKS = (2, 2, 2, 2, 4, 4, 4, 4, 4, 2, 2)
+CHUNKS = (2, 2, 4, 4, 4, 4, 4, 4, 4)
 RING = 7
 MOVES = ((4, 12), (10, 4), (2, 10), (8, 2), (0, 8), (6, 0))
 REGIONS = ((1, 0), (1, 2), (1, 1), (0, 0), (0, 1), (2, 1), (2, 2))
@@ -213,8 +213,25 @@ def tile_gpi_t_kernel(tc, x, w, b, mask, out):
         ost = {}
         acc = {}
 
+        pending = []
+        cursor = [0]
+
+        def queue_moves(m):
+            for ci in range(3, len(CHUNKS)):
+                if first_pair[ci] == m + 3:
+                    pending.extend([(ci, i) for i in range(0, 3)])
+                if first_pair[ci] == m + 2:
+                    pending.extend([(ci, i) for i in range(3, 6)])
+
+        def emit_moves(count):
+            for k in range(count):
+                ci, i = pending[cursor[0]]
+                cursor[0] += 1
+                move_x(ci, i, i + 1)
+
         def stage_t(n):
             ci, j0 = pairs[n]
+            queue_moves(n)
             for bk in range(3):
                 pt = ps_t.tile([P, 512], F32, tag="T", name="pt%d_%d" % (n, bk))
                 for sl in range(2):
@@ -231,17 +248,10 @@ def tile_gpi_t_kernel(tc, x, w, b, mask, out):
                     in_=pt[:].rearrange("p (s u r) -> p s r u", s=2, u=2),
                 )
                 grouped[(n, bk)] = grp
+                left = len(pending) - cursor[0]
+                emit_moves((left + 2 - bk) // (3 - bk))
             if j0 + 2 == CHUNKS[ci] and ci + RING < len(CHUNKS):
                 load_x(ci + RING)
-
-        def fill_moves(m):
-            for ci, jn in enumerate(CHUNKS):
-                if jn == 2 and first_pair[ci] == m + 2 and ci > 2:
-                    move_x(ci, 0, 6)
-                if jn == 4 and first_pair[ci] == m + 3:
-                    move_x(ci, 0, 3)
-                if jn == 4 and first_pair[ci] == m + 2:
-                    move_x(ci, 3, 6)
 
         def quant(n, bk):
             cod = cpool.tile([P, 256], U32, tag="c", name="c%d_%d" % (n, bk), align_bytes=64)
@@ -286,10 +296,15 @@ def tile_gpi_t_kernel(tc, x, w, b, mask, out):
             if i == 0:
                 ost[n] = opool.tile([P, 2 * N], F32, tag="o", name="o%d" % n)
             ov = ost[n][:].rearrange("p (j n) -> p j n", n=N)
+            ra = chunk_rows[ci]
+            dst = out[ra : ra + P * jn, :].rearrange("(p j) n -> p j n", j=jn)
+            last = n == n_pairs - 1
             if i < 2:
                 nc.vector.tensor_tensor(
                     out=ov[:, i, 0:512], in0=acc[(n, i)][:], in1=bias_a[:], op=ADD
                 )
+                if last:
+                    nc.sync.dma_start(out=dst[:, j0 + i, 0:512], in_=ov[:, i, 0:512])
             else:
                 nc.vector.tensor_tensor(
                     out=ov[:, :, 512:768],
@@ -297,11 +312,10 @@ def tile_gpi_t_kernel(tc, x, w, b, mask, out):
                     in1=bias_b[:].rearrange("p (t n) -> p t n", t=2),
                     op=ADD,
                 )
-                ra = chunk_rows[ci]
-                nc.sync.dma_start(
-                    out=out[ra : ra + P * jn, :].rearrange("(p j) n -> p j n", j=jn)[:, j0 : j0 + 2, :],
-                    in_=ov,
-                )
+                if last:
+                    nc.sync.dma_start(out=dst[:, j0 : j0 + 2, 512:768], in_=ov[:, :, 512:768])
+                else:
+                    nc.sync.dma_start(out=dst[:, j0 : j0 + 2, :], in_=ov)
 
         b0, b2, b1, a0, a1, c1r, c2r = REGIONS
         for reg in (b0, b2, b1):
@@ -355,14 +369,13 @@ def tile_gpi_t_kernel(tc, x, w, b, mask, out):
         x2(c1r)
         wq(c2r)
         wq(c1r)
-        move_x(1, 0, 6)
-        move_x(2, 0, 6)
+        for i in range(6):
+            move_x(1, i, i + 1)
+            move_x(2, i, i + 1)
 
         stage_mx(0, True)
         stage_t(1)
         stage_t(2)
-        fill_moves(1)
-        fill_moves(2)
         evac(0, 0)
         quant(1, 0)
         evac(0, 1)
@@ -373,7 +386,6 @@ def tile_gpi_t_kernel(tc, x, w, b, mask, out):
             stage_mx(n, False)
             if n + 2 < n_pairs:
                 stage_t(n + 2)
-                fill_moves(n + 2)
             if n + 1 < n_pairs:
                 quant(n + 1, 0)
                 quant(n + 1, 1)

@@ -193,12 +193,14 @@ def tile_gpi_t_kernel(tc, x, w, b, mask, out):
                     bank2[reg][:, i * P : (i + 1) * P], wf[:, i * P : (i + 1) * P], ident[:]
                 )
 
-        def x2(reg):
+        def x2(reg, on_vector=False):
             wgr[reg] = wpool.tile([P, 1024], BF16, name="wg%d%d" % reg, align_bytes=64)
-            nc.scalar.copy(
-                out=wgr[reg][:].bitcast(F32).rearrange("p (j e u) -> p j e u", e=2, u=2),
-                in_=bank2[reg][:].rearrange("p (e u j) -> p j e u", e=2, u=2),
-            )
+            dst = wgr[reg][:].bitcast(F32).rearrange("p (j e u) -> p j e u", e=2, u=2)
+            src = bank2[reg][:].rearrange("p (e u j) -> p j e u", e=2, u=2)
+            if on_vector:
+                nc.vector.tensor_copy(out=dst, in_=src)
+            else:
+                nc.scalar.copy(out=dst, in_=src)
 
         def wq(reg):
             r = REGIONS.index(reg)
@@ -366,7 +368,7 @@ def tile_gpi_t_kernel(tc, x, w, b, mask, out):
         t2(c2r, ps_t, "T")
         x2(c2r)
         t2(c1r, ps_t, "T")
-        x2(c1r)
+        x2(c1r, True)
         wq(c2r)
         wq(c1r)
         for i in range(6):

@@ -44,6 +44,8 @@ def tile_gpi_t_kernel(tc, x, w, b, mask, out):
         make_identity(nc, ident[:])
         ones = const.tile([P, P], BF16, name="ones")
         nc.vector.memset(ones[:], 1.0)
+        warm = const.tile([P, 512], BF16, name="warm")
+        nc.vector.memset(warm[:], 1.0)
         brow = const.tile([P, N], BF16, name="brow")
         nc.vector.memset(brow[:], 0.0)
 
@@ -87,6 +89,7 @@ def tile_gpi_t_kernel(tc, x, w, b, mask, out):
             for j0 in range(0, jn, 2):
                 pairs.append((ci, j0))
         n_pairs = len(pairs)
+        xt = {}
         xw = {}
 
         def load_x(ci):
@@ -97,12 +100,25 @@ def tile_gpi_t_kernel(tc, x, w, b, mask, out):
                 out=x_t[:].rearrange("p (j c) -> p j c", j=jn)[:, :, 0:K],
                 in_=x[ra : ra + P * jn, :].rearrange("(p j) k -> p j k", j=jn),
             )
+            xt[ci] = x_t
             xw[ci] = x_t[:].bitcast(F32)
 
         def move_x(ci, lo, hi):
             xs = xw[ci].rearrange("p (j s c) -> p j s c", j=CHUNKS[ci], s=SLOTS)
             for src, dst in MOVES[lo:hi]:
                 nc.scalar.copy(out=xs[:, :, dst, :], in_=xs[:, :, src, :])
+
+        def move_x_aside(ci):
+            xs = xt[ci][:].rearrange("p (j s c) -> p j s c", j=CHUNKS[ci], s=SLOTS)
+            for src, dst in MOVES:
+                nc.gpsimd.tensor_scalar(
+                    out=xs[:, :, dst, :],
+                    in0=xs[:, :, src, :],
+                    scalar1=1.0,
+                    scalar2=0.0,
+                    op0=MULT,
+                    op1=ADD,
+                )
 
         load_mask(0)
         load_w(0, 1)
@@ -118,7 +134,12 @@ def tile_gpi_t_kernel(tc, x, w, b, mask, out):
         for ci in range(1, RING):
             load_x(ci)
 
+        def heat(bank, count):
+            for k in range(count):
+                nc.tensor.matmul(out=bank[:], lhsT=ones[:], rhs=warm[:], start=True, stop=True)
+
         pb_a = ps_o.tile([P, 512], F32, tag="O", name="pb_a")
+        heat(pb_a, 5)
         nc.tensor.matmul(out=pb_a[:], lhsT=ones[:], rhs=brow[:, 0:512], start=True, stop=True)
         bias_a = const.tile([P, 512], F32, name="bias_a")
         nc.scalar.copy(out=bias_a[:], in_=pb_a[:])
@@ -187,6 +208,7 @@ def tile_gpi_t_kernel(tc, x, w, b, mask, out):
 
         def t2(reg, pool, tag):
             bank2[reg] = pool.tile([P, 512], F32, tag=tag, name="t2_%d%d" % reg)
+            heat(bank2[reg], 1)
             wf = wtr[reg][:].bitcast(F32)
             for i in range(4):
                 nc.tensor.transpose(
@@ -231,11 +253,12 @@ def tile_gpi_t_kernel(tc, x, w, b, mask, out):
                 cursor[0] += 1
                 move_x(ci, i, i + 1)
 
-        def stage_t(n):
+        def stage_t(n, hot=0):
             ci, j0 = pairs[n]
             queue_moves(n)
             for bk in range(3):
                 pt = ps_t.tile([P, 512], F32, tag="T", name="pt%d_%d" % (n, bk))
+                heat(pt, hot)
                 for sl in range(2):
                     t, o = divmod(2 * bk + sl, 3)
                     for u in range(2):
@@ -319,6 +342,8 @@ def tile_gpi_t_kernel(tc, x, w, b, mask, out):
                 else:
                     nc.sync.dma_start(out=dst[:, j0 : j0 + 2, :], in_=ov)
 
+        move_x_aside(1)
+        move_x_aside(2)
         b0, b2, b1, a0, a1, c1r, c2r = REGIONS
         for reg in (b0, b2, b1):
             t1(reg, 0)
@@ -328,7 +353,7 @@ def tile_gpi_t_kernel(tc, x, w, b, mask, out):
         t2(b0, ps_t, "T")
         move_x(0, 0, 6)
         x2(b0)
-        stage_t(0)
+        stage_t(0, 1)
         mult(b2, 1)
         mult(b2, 0)
         wq(b0)
@@ -371,12 +396,8 @@ def tile_gpi_t_kernel(tc, x, w, b, mask, out):
         x2(c1r, True)
         wq(c2r)
         wq(c1r)
-        for i in range(6):
-            move_x(1, i, i + 1)
-            move_x(2, i, i + 1)
-
+        stage_t(1, 1)
         stage_mx(0, True)
-        stage_t(1)
         stage_t(2)
         evac(0, 0)
         quant(1, 0)

@@ -18,6 +18,8 @@ SLOTS = 13
 ROW_W = SLOTS * HB
 CHUNKS = (2, 2, 4, 4, 4, 4, 4, 4, 4)
 RING = 7
+LATE = 3
+RUN = 4
 MOVES = ((4, 12), (10, 4), (2, 10), (8, 2), (0, 8), (6, 0))
 REGIONS = ((1, 0), (1, 2), (1, 1), (0, 0), (0, 1), (2, 1), (2, 2))
 COLS = ((0, 512), (0, 768), (256, 768))
@@ -35,7 +37,7 @@ def tile_gpi_t_kernel(tc, x, w, b, mask, out):
         xpool = ctx.enter_context(tc.tile_pool(name="xpool", bufs=RING))
         gpool = ctx.enter_context(tc.tile_pool(name="gpool", bufs=6))
         cpool = ctx.enter_context(tc.tile_pool(name="cpool", bufs=9))
-        opool = ctx.enter_context(tc.tile_pool(name="opool", bufs=5))
+        opool = ctx.enter_context(tc.tile_pool(name="opool", bufs=8))
         ps_t = ctx.enter_context(tc.psum_pool(name="ps_t", bufs=4))
         ps_o = ctx.enter_context(tc.psum_pool(name="ps_o", bufs=4))
         ctx.enter_context(tc.manual_schedule())
@@ -124,8 +126,8 @@ def tile_gpi_t_kernel(tc, x, w, b, mask, out):
         load_w(0, 1)
         nc.sync.dma_start(out=brow[0:1, :], in_=b.rearrange("(o n) -> o n", o=1))
         load_w(1, 1)
-        load_x(0)
         load_mask(2)
+        load_x(0)
         load_mask(1)
         load_w(0, 0)
         load_w(1, 0)
@@ -183,10 +185,11 @@ def tile_gpi_t_kernel(tc, x, w, b, mask, out):
             wv = wtr[reg][:].rearrange("p (e l k) -> p e l k", e=2, l=4)
             return bv, wv
 
-        def ones_copy(reg, s):
-            bv, wv = views(reg)
-            lo = 0 if s == 1 else 1
-            nc.scalar.copy(out=wv[:, :, lo:4:2, :], in_=bv[:, :, lo:4:2, :])
+        def ones_copy(reg):
+            nc.scalar.copy(
+                out=wtr[reg][:].rearrange("p (e c) -> p e c", e=2),
+                in_=bank1[reg][:].bitcast(BF16).rearrange("p (c e) -> p e c", e=2),
+            )
 
         def mult(reg, s):
             o, ub = reg
@@ -237,62 +240,43 @@ def tile_gpi_t_kernel(tc, x, w, b, mask, out):
         ost = {}
         acc = {}
 
-        pending = []
-        cursor = [0]
-
-        def queue_moves(m):
-            for ci in range(3, len(CHUNKS)):
-                if first_pair[ci] == m + 3:
-                    pending.extend([(ci, i) for i in range(0, 3)])
-                if first_pair[ci] == m + 2:
-                    pending.extend([(ci, i) for i in range(3, 6)])
-
-        def emit_moves(count):
-            for k in range(count):
-                ci, i = pending[cursor[0]]
-                cursor[0] += 1
-                move_x(ci, i, i + 1)
-
-        def stage_t(n, hot=0):
+        def t_unit(k, hot=0):
+            n, bk = divmod(k, 3)
             ci, j0 = pairs[n]
-            queue_moves(n)
-            for bk in range(3):
-                pt = ps_t.tile([P, 512], F32, tag="T", name="pt%d_%d" % (n, bk))
-                heat(pt, hot)
-                for sl in range(2):
-                    t, o = divmod(2 * bk + sl, 3)
-                    for u in range(2):
-                        off = (j0 + t) * ROW_W + HB * (2 * o + 7 * u)
-                        i = 2 * sl + u
-                        nc.tensor.transpose(
-                            pt[:, i * P : (i + 1) * P], xw[ci][:, off : off + P], ident[:]
-                        )
-                grp = gpool.tile([P, 1024], BF16, tag="g", name="g%d_%d" % (n, bk), align_bytes=64)
-                nc.scalar.copy(
-                    out=grp[:].bitcast(F32).rearrange("p (s r u) -> p s r u", s=2, u=2),
-                    in_=pt[:].rearrange("p (s u r) -> p s r u", s=2, u=2),
-                )
-                grouped[(n, bk)] = grp
-                left = len(pending) - cursor[0]
-                emit_moves((left + 2 - bk) // (3 - bk))
-            if j0 + 2 == CHUNKS[ci] and ci + RING < len(CHUNKS):
+            pt = ps_t.tile([P, 512], F32, tag="T", name="pt%d_%d" % (n, bk))
+            heat(pt, hot)
+            for sl in range(2):
+                t, o = divmod(2 * bk + sl, 3)
+                for u in range(2):
+                    off = (j0 + t) * ROW_W + HB * (2 * o + 7 * u)
+                    i = 2 * sl + u
+                    nc.tensor.transpose(
+                        pt[:, i * P : (i + 1) * P], xw[ci][:, off : off + P], ident[:]
+                    )
+            grp = gpool.tile([P, 1024], BF16, tag="g", name="g%d_%d" % (n, bk), align_bytes=64)
+            nc.scalar.copy(
+                out=grp[:].bitcast(F32).rearrange("p (s r u) -> p s r u", s=2, u=2),
+                in_=pt[:].rearrange("p (s u r) -> p s r u", s=2, u=2),
+            )
+            grouped[k] = grp
+            for c2 in range(3, len(CHUNKS)):
+                i = k - 3 * first_pair[c2] + 9
+                if 0 <= i < 6:
+                    move_x(c2, i, i + 1)
+            if bk == 2 and j0 + 2 == CHUNKS[ci] and ci + RING < len(CHUNKS):
                 load_x(ci + RING)
 
-        def quant(n, bk):
-            cod = cpool.tile([P, 256], U32, tag="c", name="c%d_%d" % (n, bk), align_bytes=64)
-            scl = cpool.tile([P, 256], U8, tag="s", name="s%d_%d" % (n, bk), align_bytes=64)
-            nc.vector.quantize_mx(out=cod[:].bitcast(FP8X4), scales=scl[:], in_=grouped[(n, bk)][:])
-            codes[(n, bk)] = (cod, scl)
+        def quant(k):
+            cod = cpool.tile([P, 256], U32, tag="c", name="c%d" % k, align_bytes=64)
+            scl = cpool.tile([P, 256], U8, tag="s", name="s%d" % k, align_bytes=64)
+            nc.vector.quantize_mx(out=cod[:].bitcast(FP8X4), scales=scl[:], in_=grouped[k][:])
+            codes[k] = (cod, scl)
 
-        def one_pass(n, t, ub, o):
+        def one_pass(n, t, ub, o, dst):
             ops = OPS_OF_UB[ub]
             bk, sl = divmod(3 * t + o, 2)
-            cod, scl = codes[(n, bk)]
+            cod, scl = codes[3 * n + bk]
             r = REGIONS.index((o, ub))
-            if ub == 2:
-                dst = acc[(n, 2)][:, 256 * t : 256 * t + 256]
-            else:
-                dst = acc[(n, t)][:, 256 * ub : 256 * ub + 256]
             nc.tensor.matmul_mx(
                 out=dst,
                 lhsT=cod[:, sl * P : (sl + 1) * P].bitcast(FP8X4),
@@ -303,33 +287,49 @@ def tile_gpi_t_kernel(tc, x, w, b, mask, out):
                 stop=(o == ops[-1]),
             )
 
-        def stage_mx(n, late_c):
-            for i in range(3):
-                acc[(n, i)] = ps_o.tile([P, 512], F32, tag="O", name="acc%d_%d" % (n, i))
-            if late_c:
-                order = [(0, 0, 0), (0, 0, 1), (0, 1, 0), (0, 1, 1), (1, 0, 0), (1, 0, 1), (1, 1, 0), (1, 1, 1)]
-                order += [(0, 2, 1), (0, 1, 2), (1, 1, 2), (0, 2, 2), (1, 2, 1), (1, 2, 2)]
-            else:
-                order = [(t, ub, o) for t in range(2) for ub in range(2) for o in OPS_OF_UB[ub]]
-                order += [(t, 2, o) for t in range(2) for o in OPS_OF_UB[2]]
-            for t, ub, o in order:
-                one_pass(n, t, ub, o)
+        def acc_part(n, t, ub):
+            if ub == 2:
+                return acc[(n, 2)][:, 256 * t : 256 * t + 256]
+            return acc[(n, t)][:, 256 * ub : 256 * ub + 256]
 
-        def evac(n, i):
+        def new_acc(n, i):
+            acc[(n, i)] = ps_o.tile([P, 512], F32, tag="O", name="acc%d_%d" % (n, i))
+
+        def mx_first():
+            for i in range(3):
+                new_acc(0, i)
+            order = [(t, ub, o) for t in range(2) for ub in range(2) for o in range(2)]
+            order += [(0, 2, 1), (0, 1, 2), (1, 1, 2), (0, 2, 2), (1, 2, 1), (1, 2, 2)]
+            for t, ub, o in order:
+                one_pass(0, t, ub, o, acc_part(0, t, ub))
+
+        def mx_unit(k):
+            n, i = divmod(k, 3)
+            new_acc(n, i)
+            for t, ub in (((0, 2), (1, 2)) if i == 2 else ((i, 0), (i, 1))):
+                for o in OPS_OF_UB[ub]:
+                    one_pass(n, t, ub, o, acc_part(n, t, ub))
+
+        def out_rows(n):
             ci, j0 = pairs[n]
             jn = CHUNKS[ci]
-            if i == 0:
-                ost[n] = opool.tile([P, 2 * N], F32, tag="o", name="o%d" % n)
-            ov = ost[n][:].rearrange("p (j n) -> p j n", n=N)
             ra = chunk_rows[ci]
             dst = out[ra : ra + P * jn, :].rearrange("(p j) n -> p j n", j=jn)
-            last = n == n_pairs - 1
+            return dst[:, j0 : j0 + 2, :]
+
+        def evac(k):
+            n, i = divmod(k, 3)
+            if n not in ost:
+                ost[n] = opool.tile([P, 2 * N], F32, tag="o", name="o%d" % n)
+            ov = ost[n][:].rearrange("p (j n) -> p j n", n=N)
+            late = n >= n_pairs - LATE
+            dst = out_rows(n)
             if i < 2:
                 nc.vector.tensor_tensor(
                     out=ov[:, i, 0:512], in0=acc[(n, i)][:], in1=bias_a[:], op=ADD
                 )
-                if last:
-                    nc.sync.dma_start(out=dst[:, j0 + i, 0:512], in_=ov[:, i, 0:512])
+                if late:
+                    nc.sync.dma_start(out=dst[:, i, 0:512], in_=ov[:, i, 0:512])
             else:
                 nc.vector.tensor_tensor(
                     out=ov[:, :, 512:768],
@@ -337,55 +337,76 @@ def tile_gpi_t_kernel(tc, x, w, b, mask, out):
                     in1=bias_b[:].rearrange("p (t n) -> p t n", t=2),
                     op=ADD,
                 )
-                if last:
-                    nc.sync.dma_start(out=dst[:, j0 : j0 + 2, 512:768], in_=ov[:, :, 512:768])
+                if late:
+                    nc.sync.dma_start(out=dst[:, :, 512:768], in_=ov[:, :, 512:768])
                 else:
-                    nc.sync.dma_start(out=dst[:, j0 : j0 + 2, :], in_=ov)
+                    nc.sync.dma_start(out=dst, in_=ov)
 
+        def last_pair():
+            n = n_pairs - 1
+            dst = out_rows(n)
+            ost[n] = opool.tile([P, 2 * N], F32, tag="o", name="o%d" % n)
+            ov = ost[n][:].rearrange("p (j n) -> p j n", n=N)
+            mx_unit(3 * n + 2)
+            evac(3 * n + 2)
+            mx_unit(3 * n)
+            evac(3 * n)
+            for ub in (1, 0):
+                part = ps_t.tile([P, 512], F32, tag="T", name="end%d" % ub)
+                cols = slice(256 * ub, 256 * ub + 256)
+                for o in OPS_OF_UB[ub]:
+                    one_pass(n, 1, ub, o, part[:, 0:256])
+                nc.vector.tensor_tensor(
+                    out=ov[:, 1, cols], in0=part[:, 0:256], in1=bias_a[:, cols], op=ADD
+                )
+                nc.sync.dma_start(out=dst[:, 1, cols], in_=ov[:, 1, cols])
+
+        b0, b2, b1, a0, a1, c1r, c2r = REGIONS
         move_x_aside(1)
         move_x_aside(2)
-        b0, b2, b1, a0, a1, c1r, c2r = REGIONS
-        for reg in (b0, b2, b1):
-            t1(reg, 0)
-            t1(reg, 1)
+        t1(b0, 0)
+        t1(b0, 1)
+        t1(b2, 0)
+        t1(b2, 1)
+        t1(b1, 0)
+        t1(b1, 1)
         mult(b0, 1)
         mult(b0, 0)
         t2(b0, ps_t, "T")
         move_x(0, 0, 6)
         x2(b0)
-        stage_t(0, 1)
+        for k in range(3):
+            t_unit(k, 1)
         mult(b2, 1)
         mult(b2, 0)
         wq(b0)
-        quant(0, 0)
+        quant(0)
         t2(b2, ps_t, "T")
         x2(b2)
         mult(b1, 1)
         mult(b1, 0)
-        quant(0, 1)
-        quant(0, 2)
+        quant(1)
+        quant(2)
         wq(b2)
         t1(a0, 0)
         t1(a1, 0)
         t1(a0, 1)
         t1(a1, 1)
         t2(b1, ps_t, "T")
-        ones_copy(a0, 0)
-        ones_copy(a0, 1)
+        ones_copy(a0)
         x2(b1)
-        mult(a1, 0)
         mult(a1, 1)
+        mult(a1, 0)
         wq(b1)
         t1(c2r, 0)
         t1(c1r, 0)
         t2(a0, ps_t, "T")
         t1(c2r, 1)
         t1(c1r, 1)
-        ones_copy(c2r, 0)
+        ones_copy(c2r)
         x2(a0)
-        ones_copy(c2r, 1)
-        mult(c1r, 0)
         mult(c1r, 1)
+        mult(c1r, 0)
         wq(a0)
         t2(a1, ps_t, "T")
         x2(a1)
@@ -396,24 +417,31 @@ def tile_gpi_t_kernel(tc, x, w, b, mask, out):
         x2(c1r, True)
         wq(c2r)
         wq(c1r)
-        stage_t(1, 1)
-        stage_mx(0, True)
-        stage_t(2)
-        evac(0, 0)
-        quant(1, 0)
-        evac(0, 1)
-        quant(1, 1)
-        evac(0, 2)
-        quant(1, 2)
-        for n in range(1, n_pairs):
-            stage_mx(n, False)
-            if n + 2 < n_pairs:
-                stage_t(n + 2)
-            if n + 1 < n_pairs:
-                quant(n + 1, 0)
-                quant(n + 1, 1)
-            evac(n, 0)
-            if n + 1 < n_pairs:
-                quant(n + 1, 2)
-            evac(n, 1)
-            evac(n, 2)
+
+        n_units = 3 * n_pairs
+        for k in range(3, 6):
+            t_unit(k, 1)
+            quant(k)
+        mx_first()
+        evac(0)
+        evac(1)
+        evac(2)
+        for k in range(6, 6 + RUN):
+            t_unit(k)
+        done_t = 6 + RUN
+        done_q = 6
+        for k0 in range(3, n_units - 3, RUN):
+            ks = range(k0, min(k0 + RUN, n_units - 3))
+            if done_q < done_t:
+                quant(done_q)
+                done_q += 1
+            for k in ks:
+                mx_unit(k)
+                if done_q < done_t:
+                    quant(done_q)
+                    done_q += 1
+                evac(k)
+            for k in range(done_t, min(done_t + RUN, n_units)):
+                t_unit(k)
+            done_t = min(done_t + RUN, n_units)
+        last_pair()

@@ -19,7 +19,7 @@ ROW_W = SLOTS * HB
 CHUNKS = (2, 2, 4, 4, 4, 4, 4, 4, 4)
 RING = 7
 LATE = 3
-RUN = 4
+RUN = 3
 MOVES = ((4, 12), (10, 4), (2, 10), (8, 2), (0, 8), (6, 0))
 REGIONS = ((1, 0), (1, 2), (1, 1), (0, 0), (0, 1), (2, 1), (2, 2))
 COLS = ((0, 512), (0, 768), (256, 768))

@@ -16,8 +16,8 @@ P = 128
 HB = 64
 SLOTS = 13
 ROW_W = SLOTS * HB
-CHUNKS = (2, 2, 4, 4, 4, 4, 4, 4, 4)
-RING = 7
+CHUNKS = (2, 2, 2, 2, 4, 4, 4, 4, 4, 4)
+RING = 6
 LATE = 3
 RUN = 3
 MOVES = ((4, 12), (10, 4), (2, 10), (8, 2), (0, 8), (6, 0))
@@ -35,6 +35,7 @@ def tile_gpi_t_kernel(tc, x, w, b, mask, out):
         const = ctx.enter_context(tc.tile_pool(name="const", bufs=1))
         wpool = ctx.enter_context(tc.tile_pool(name="wpool", bufs=1))
         xpool = ctx.enter_context(tc.tile_pool(name="xpool", bufs=RING))
+        oddpool = ctx.enter_context(tc.tile_pool(name="oddpool", bufs=3))
         gpool = ctx.enter_context(tc.tile_pool(name="gpool", bufs=6))
         cpool = ctx.enter_context(tc.tile_pool(name="cpool", bufs=9))
         opool = ctx.enter_context(tc.tile_pool(name="opool", bufs=8))
@@ -91,7 +92,7 @@ def tile_gpi_t_kernel(tc, x, w, b, mask, out):
             for j0 in range(0, jn, 2):
                 pairs.append((ci, j0))
         n_pairs = len(pairs)
-        xt = {}
+        xodd = {}
         xw = {}
 
         def load_x(ci):
@@ -102,7 +103,6 @@ def tile_gpi_t_kernel(tc, x, w, b, mask, out):
                 out=x_t[:].rearrange("p (j c) -> p j c", j=jn)[:, :, 0:K],
                 in_=x[ra : ra + P * jn, :].rearrange("(p j) k -> p j k", j=jn),
             )
-            xt[ci] = x_t
             xw[ci] = x_t[:].bitcast(F32)
 
         def move_x(ci, lo, hi):
@@ -110,24 +110,23 @@ def tile_gpi_t_kernel(tc, x, w, b, mask, out):
             for src, dst in MOVES[lo:hi]:
                 nc.scalar.copy(out=xs[:, :, dst, :], in_=xs[:, :, src, :])
 
-        def move_x_aside(ci):
-            xs = xt[ci][:].rearrange("p (j s c) -> p j s c", j=CHUNKS[ci], s=SLOTS)
-            for src, dst in MOVES:
-                nc.gpsimd.tensor_scalar(
-                    out=xs[:, :, dst, :],
-                    in0=xs[:, :, src, :],
-                    scalar1=1.0,
-                    scalar2=0.0,
-                    op0=MULT,
-                    op1=ADD,
-                )
+        def move_three(ci, on_vector):
+            jn = CHUNKS[ci]
+            odd_t = oddpool.tile([P, jn * 6 * HB], F32, tag="odd", name="odd%d" % ci)
+            xs = xw[ci].rearrange("p (j s c) -> p j s c", j=jn, s=SLOTS)
+            od = odd_t[:].rearrange("p (j s c) -> p j s c", j=jn, s=6)
+            copy = nc.vector.tensor_copy if on_vector else nc.scalar.copy
+            copy(out=od[:, :, 1:6:2, :], in_=xs[:, :, 0:6:2, :])
+            copy(out=od[:, :, 0:6:2, :], in_=xs[:, :, 7:12:2, :])
+            copy(out=xs[:, :, 0:6:2, :], in_=xs[:, :, 6:12:2, :])
+            xodd[ci] = odd_t[:]
 
         load_mask(0)
         load_w(0, 1)
         nc.sync.dma_start(out=brow[0:1, :], in_=b.rearrange("(o n) -> o n", o=1))
         load_w(1, 1)
-        load_mask(2)
         load_x(0)
+        load_mask(2)
         load_mask(1)
         load_w(0, 0)
         load_w(1, 0)
@@ -159,6 +158,12 @@ def tile_gpi_t_kernel(tc, x, w, b, mask, out):
 
         wc = wpool.tile([P, 7 * 256], U32, name="wc", align_bytes=64)
         wsc = wpool.tile([P, 7 * 256], U8, name="wsc", align_bytes=64)
+        pick = const.tile([P, 2, 192], BF16, name="pick")
+        nc.gpsimd.memset(pick[:], 0.0)
+        nc.gpsimd.tensor_copy(
+            out=pick[:, :, 64:128], in_=ident[:].rearrange("p (m e) -> p e m", e=2)
+        )
+        spread = {}
         bank1 = {}
         bank2 = {}
         wtr = {}
@@ -185,11 +190,33 @@ def tile_gpi_t_kernel(tc, x, w, b, mask, out):
             wv = wtr[reg][:].rearrange("p (e l k) -> p e l k", e=2, l=4)
             return bv, wv
 
-        def ones_copy(reg):
-            nc.scalar.copy(
-                out=wtr[reg][:].rearrange("p (e c) -> p e c", e=2),
-                in_=bank1[reg][:].bitcast(BF16).rearrange("p (c e) -> p e c", e=2),
-            )
+        def spread_ones(reg, h, pool, tag):
+            o, ub = reg
+            c0, c1 = COLS[o]
+            bank = pool.tile([P, 512], F32, tag=tag, name="so%d%d_%d" % (o, ub, h))
+            for u in range(2):
+                for e in range(2):
+                    q = 2 * u + e
+                    for i, (s, us) in enumerate(ORDER[2 * u : 2 * u + 2]):
+                        off = us * (c1 - c0) + 256 * ub - c0 + P * h
+                        nc.tensor.matmul(
+                            out=bank[:, q * P : (q + 1) * P],
+                            lhsT=pick[:, e, 64 - 64 * i : 192 - 64 * i],
+                            rhs=wt[(s, o)][:, off : off + P],
+                            start=(i == 0),
+                            stop=(i == 1),
+                        )
+            spread[(reg, h)] = bank
+
+        def ones_out(reg, h, on_vector=False):
+            if h == 0:
+                wgr[reg] = wpool.tile([P, 1024], BF16, name="wg%d%d" % reg, align_bytes=64)
+            dst = wgr[reg][:, 512 * h : 512 * h + 512].rearrange("p (n q) -> p n q", q=4)
+            src = spread[(reg, h)][:].rearrange("p (q n) -> p n q", q=4)
+            if on_vector:
+                nc.vector.tensor_copy(out=dst, in_=src)
+            else:
+                nc.scalar.copy(out=dst, in_=src)
 
         def mult(reg, s):
             o, ub = reg
@@ -248,19 +275,22 @@ def tile_gpi_t_kernel(tc, x, w, b, mask, out):
             for sl in range(2):
                 t, o = divmod(2 * bk + sl, 3)
                 for u in range(2):
-                    off = (j0 + t) * ROW_W + HB * (2 * o + 7 * u)
+                    if u == 1 and ci in xodd:
+                        off = (j0 + t) * 6 * HB + HB * 2 * o
+                        words = xodd[ci][:, off : off + P]
+                    else:
+                        off = (j0 + t) * ROW_W + HB * (2 * o + 7 * u)
+                        words = xw[ci][:, off : off + P]
                     i = 2 * sl + u
-                    nc.tensor.transpose(
-                        pt[:, i * P : (i + 1) * P], xw[ci][:, off : off + P], ident[:]
-                    )
+                    nc.tensor.transpose(pt[:, i * P : (i + 1) * P], words, ident[:])
             grp = gpool.tile([P, 1024], BF16, tag="g", name="g%d_%d" % (n, bk), align_bytes=64)
             nc.scalar.copy(
                 out=grp[:].bitcast(F32).rearrange("p (s r u) -> p s r u", s=2, u=2),
                 in_=pt[:].rearrange("p (s u r) -> p s r u", s=2, u=2),
             )
             grouped[k] = grp
-            for c2 in range(3, len(CHUNKS)):
-                i = k - 3 * first_pair[c2] + 9
+            for c2 in range(4, len(CHUNKS)):
+                i = k - 3 * first_pair[c2] + 7
                 if 0 <= i < 6:
                     move_x(c2, i, i + 1)
             if bk == 2 and j0 + 2 == CHUNKS[ci] and ci + RING < len(CHUNKS):
@@ -295,11 +325,14 @@ def tile_gpi_t_kernel(tc, x, w, b, mask, out):
         def new_acc(n, i):
             acc[(n, i)] = ps_o.tile([P, 512], F32, tag="O", name="acc%d_%d" % (n, i))
 
-        def mx_first():
-            for i in range(3):
-                new_acc(0, i)
-            order = [(t, ub, o) for t in range(2) for ub in range(2) for o in range(2)]
-            order += [(0, 2, 1), (0, 1, 2), (1, 1, 2), (0, 2, 2), (1, 2, 1), (1, 2, 2)]
+        def mx_first(late):
+            if late:
+                order = [(0, 1, 2), (1, 1, 2)]
+                order += [(t, 2, o) for t in range(2) for o in (1, 2)]
+            else:
+                for i in range(3):
+                    new_acc(0, i)
+                order = [(t, ub, o) for t in range(2) for ub in range(2) for o in range(2)]
             for t, ub, o in order:
                 one_pass(0, t, ub, o, acc_part(0, t, ub))
 
@@ -362,8 +395,6 @@ def tile_gpi_t_kernel(tc, x, w, b, mask, out):
                 nc.sync.dma_start(out=dst[:, 1, cols], in_=ov[:, 1, cols])
 
         b0, b2, b1, a0, a1, c1r, c2r = REGIONS
-        move_x_aside(1)
-        move_x_aside(2)
         t1(b0, 0)
         t1(b0, 1)
         t1(b2, 0)
@@ -373,7 +404,7 @@ def tile_gpi_t_kernel(tc, x, w, b, mask, out):
         mult(b0, 1)
         mult(b0, 0)
         t2(b0, ps_t, "T")
-        move_x(0, 0, 6)
+        move_three(0, True)
         x2(b0)
         for k in range(3):
             t_unit(k, 1)
@@ -388,41 +419,43 @@ def tile_gpi_t_kernel(tc, x, w, b, mask, out):
         quant(1)
         quant(2)
         wq(b2)
-        t1(a0, 0)
+        spread_ones(a0, 0, ps_o, "O")
+        spread_ones(a0, 1, ps_o, "O")
         t1(a1, 0)
-        t1(a0, 1)
         t1(a1, 1)
         t2(b1, ps_t, "T")
-        ones_copy(a0)
+        ones_out(a0, 0)
+        ones_out(a0, 1)
         x2(b1)
         mult(a1, 1)
         mult(a1, 0)
         wq(b1)
-        t1(c2r, 0)
+        spread_ones(c2r, 0, ps_o, "O")
+        spread_ones(c2r, 1, ps_o, "O")
         t1(c1r, 0)
-        t2(a0, ps_t, "T")
-        t1(c2r, 1)
         t1(c1r, 1)
-        ones_copy(c2r)
-        x2(a0)
+        t2(a1, ps_t, "T")
+        ones_out(c2r, 0)
+        ones_out(c2r, 1)
         mult(c1r, 1)
         mult(c1r, 0)
         wq(a0)
-        t2(a1, ps_t, "T")
         x2(a1)
         wq(a1)
-        t2(c2r, ps_t, "T")
-        x2(c2r)
         t2(c1r, ps_t, "T")
-        x2(c1r, True)
+        x2(c1r)
+        move_three(1, True)
         wq(c2r)
         wq(c1r)
+        move_three(2, True)
+        move_three(3, True)
 
         n_units = 3 * n_pairs
+        mx_first(False)
         for k in range(3, 6):
-            t_unit(k, 1)
+            t_unit(k, 0)
             quant(k)
-        mx_first()
+        mx_first(True)
         evac(0)
         evac(1)
         evac(2)

@@ -14,15 +14,15 @@ MULT = mybir.AluOpType.mult
 ROWS, K, N = 4096, 1536, 768
 P = 128
 HB = 64
-SLOTS = 13
+SLOTS = 12
 ROW_W = SLOTS * HB
 CHUNKS = (2, 2, 2, 2, 4, 4, 4, 4, 4, 4)
 RING = 6
 LATE = 3
 RUN = 3
-MOVES = ((4, 12), (10, 4), (2, 10), (8, 2), (0, 8), (6, 0))
+MOVES = ((11, 12), (4, 13), (10, 4), (2, 10), (8, 2), (0, 8), (6, 0))
 REGIONS = ((1, 0), (1, 2), (1, 1), (0, 0), (0, 1), (2, 1), (2, 2))
-COLS = ((0, 512), (0, 768), (256, 768))
+COLS = (((0, 512),), ((0, 768),), ((256, 768),))
 OPS_OF_UB = ((0, 1), (0, 1, 2), (1, 2))
 
 FLOPS = 2 * ROWS * K * N
@@ -73,13 +73,19 @@ def tile_gpi_t_kernel(tc, x, w, b, mask, out):
                 )
             mask_sb[ub] = m_t
 
-        def load_w(s, o):
-            c0, c1 = COLS[o]
-            w_t = wpool.tile([P, 2 * (c1 - c0)], BF16, name="w%d%d" % (s, o))
+        def load_w(s, o, part=0):
+            c0, c1 = COLS[o][part]
+            w_t = wpool.tile([P, 2 * (c1 - c0)], BF16, name="w%d%d%d" % (s, o, part))
             nc.sync.dma_start(
                 out=w_t[:].rearrange("p (u n) -> p u n", u=2), in_=w_v[s, o][:, :, c0:c1]
             )
-            wt[(s, o)] = w_t
+            wt[(s, o, part)] = w_t
+
+        def w_at(s, reg):
+            o, ub = reg
+            for part, (c0, c1) in enumerate(COLS[o]):
+                if c0 <= 256 * ub < c1:
+                    return wt[(s, o, part)], c1 - c0, 256 * ub - c0
 
         chunk_rows = []
         first_pair = []
@@ -97,23 +103,34 @@ def tile_gpi_t_kernel(tc, x, w, b, mask, out):
 
         def load_x(ci):
             jn = CHUNKS[ci]
-            x_t = xpool.tile([P, jn * ROW_W * 2], BF16, tag="x", name="x%d" % ci)
+            x_t = xpool.tile([P, jn * (ROW_W + 2 * HB) * 2], BF16, tag="x", name="x%d" % ci)
             ra = chunk_rows[ci]
             nc.sync.dma_start(
-                out=x_t[:].rearrange("p (j c) -> p j c", j=jn)[:, :, 0:K],
+                out=x_t[:, 0 : jn * K].rearrange("p (j c) -> p j c", j=jn),
                 in_=x[ra : ra + P * jn, :].rearrange("(p j) k -> p j k", j=jn),
             )
             xw[ci] = x_t[:].bitcast(F32)
 
+        def row_words(ci):
+            jn = CHUNKS[ci]
+            return xw[ci][:, 0 : jn * ROW_W].rearrange("p (j s c) -> p j s c", j=jn, s=SLOTS)
+
         def move_x(ci, lo, hi):
-            xs = xw[ci].rearrange("p (j s c) -> p j s c", j=CHUNKS[ci], s=SLOTS)
+            jn = CHUNKS[ci]
+            xs = row_words(ci)
+            beside = xw[ci][:, jn * ROW_W : jn * (ROW_W + 2 * HB)].rearrange(
+                "p (j s c) -> p j s c", j=jn, s=2
+            )
             for src, dst in MOVES[lo:hi]:
-                nc.scalar.copy(out=xs[:, :, dst, :], in_=xs[:, :, src, :])
+                if dst < SLOTS:
+                    nc.scalar.copy(out=xs[:, :, dst, :], in_=xs[:, :, src, :])
+                else:
+                    nc.scalar.copy(out=beside[:, :, dst - SLOTS, :], in_=xs[:, :, src, :])
 
         def move_three(ci, on_vector):
             jn = CHUNKS[ci]
             odd_t = oddpool.tile([P, jn * 6 * HB], F32, tag="odd", name="odd%d" % ci)
-            xs = xw[ci].rearrange("p (j s c) -> p j s c", j=jn, s=SLOTS)
+            xs = row_words(ci)
             od = odd_t[:].rearrange("p (j s c) -> p j s c", j=jn, s=6)
             copy = nc.vector.tensor_copy if on_vector else nc.scalar.copy
             copy(out=od[:, :, 1:6:2, :], in_=xs[:, :, 0:6:2, :])
@@ -171,17 +188,16 @@ def tile_gpi_t_kernel(tc, x, w, b, mask, out):
         ORDER = ((1, 0), (0, 1), (1, 1), (0, 0))
 
         def t1(reg, s):
-            o, ub = reg
             if reg not in bank1:
                 bank1[reg] = ps_o.tile([P, 512], F32, tag="O", name="t1_%d%d" % reg)
                 wtr[reg] = wpool.tile([P, 1024], BF16, name="wtr%d%d" % reg)
-            c0, c1 = COLS[o]
+            w_t, width, c = w_at(s, reg)
             for slot, (s_, u) in enumerate(ORDER):
                 if s_ == s:
-                    off = (u * (c1 - c0) + ub * 256 - c0) // 2
+                    off = (u * width + c) // 2
                     nc.tensor.transpose(
                         bank1[reg][:, slot * P : (slot + 1) * P],
-                        wt[(s, o)][:].bitcast(F32)[:, off : off + P],
+                        w_t[:].bitcast(F32)[:, off : off + P],
                         ident[:],
                     )
 
@@ -192,17 +208,17 @@ def tile_gpi_t_kernel(tc, x, w, b, mask, out):
 
         def spread_ones(reg, h, pool, tag):
             o, ub = reg
-            c0, c1 = COLS[o]
             bank = pool.tile([P, 512], F32, tag=tag, name="so%d%d_%d" % (o, ub, h))
             for u in range(2):
                 for e in range(2):
                     q = 2 * u + e
                     for i, (s, us) in enumerate(ORDER[2 * u : 2 * u + 2]):
-                        off = us * (c1 - c0) + 256 * ub - c0 + P * h
+                        w_t, width, c = w_at(s, reg)
+                        off = us * width + c + P * h
                         nc.tensor.matmul(
                             out=bank[:, q * P : (q + 1) * P],
                             lhsT=pick[:, e, 64 - 64 * i : 192 - 64 * i],
-                            rhs=wt[(s, o)][:, off : off + P],
+                            rhs=w_t[:, off : off + P],
                             start=(i == 0),
                             stop=(i == 1),
                         )
@@ -280,6 +296,8 @@ def tile_gpi_t_kernel(tc, x, w, b, mask, out):
                         words = xodd[ci][:, off : off + P]
                     else:
                         off = (j0 + t) * ROW_W + HB * (2 * o + 7 * u)
+                        if (o, u) == (2, 1):
+                            off = CHUNKS[ci] * ROW_W + (j0 + t) * 2 * HB
                         words = xw[ci][:, off : off + P]
                     i = 2 * sl + u
                     nc.tensor.transpose(pt[:, i * P : (i + 1) * P], words, ident[:])
@@ -292,7 +310,7 @@ def tile_gpi_t_kernel(tc, x, w, b, mask, out):
             for c2 in range(4, len(CHUNKS)):
                 i = k - 3 * first_pair[c2] + 7
                 if 0 <= i < 6:
-                    move_x(c2, i, i + 1)
+                    move_x(c2, i + min(i, 1), i + 2)
             if bk == 2 and j0 + 2 == CHUNKS[ci] and ci + RING < len(CHUNKS):
                 load_x(ci + RING)
 
@@ -304,6 +322,8 @@ def tile_gpi_t_kernel(tc, x, w, b, mask, out):
 
         def one_pass(n, t, ub, o, dst):
             ops = OPS_OF_UB[ub]
+            if (n, ub) == (0, 1):
+                ops = (1, 0, 2)
             bk, sl = divmod(3 * t + o, 2)
             cod, scl = codes[3 * n + bk]
             r = REGIONS.index((o, ub))
@@ -325,14 +345,16 @@ def tile_gpi_t_kernel(tc, x, w, b, mask, out):
         def new_acc(n, i):
             acc[(n, i)] = ps_o.tile([P, 512], F32, tag="O", name="acc%d_%d" % (n, i))
 
-        def mx_first(late):
-            if late:
-                order = [(0, 1, 2), (1, 1, 2)]
-                order += [(t, 2, o) for t in range(2) for o in (1, 2)]
-            else:
+        def mx_first(part):
+            if part == 0:
                 for i in range(3):
                     new_acc(0, i)
-                order = [(t, ub, o) for t in range(2) for ub in range(2) for o in range(2)]
+                order = [(t, 0, o) for t in range(2) for o in range(2)]
+            elif part == 1:
+                order = [(t, 1, o) for t in range(2) for o in (1, 0)]
+            else:
+                order = [(0, 1, 2), (1, 1, 2)]
+                order += [(t, 2, o) for t in range(2) for o in (1, 2)]
             for t, ub, o in order:
                 one_pass(0, t, ub, o, acc_part(0, t, ub))
 
@@ -437,9 +459,10 @@ def tile_gpi_t_kernel(tc, x, w, b, mask, out):
         t2(a1, ps_t, "T")
         ones_out(c2r, 0)
         ones_out(c2r, 1)
+        wq(a0)
         mult(c1r, 1)
         mult(c1r, 0)
-        wq(a0)
+        mx_first(0)
         x2(a1)
         wq(a1)
         t2(c1r, ps_t, "T")
@@ -451,11 +474,11 @@ def tile_gpi_t_kernel(tc, x, w, b, mask, out):
         move_three(3, True)
 
         n_units = 3 * n_pairs
-        mx_first(False)
+        mx_first(1)
         for k in range(3, 6):
             t_unit(k, 0)
             quant(k)
-        mx_first(True)
+        mx_first(2)
         evac(0)
         evac(1)
         evac(2)

from contextlib import ExitStack

import concourse.mybir as mybir
from concourse.masks import make_identity

F32 = mybir.dt.float32
BF16 = mybir.dt.bfloat16
U32 = mybir.dt.uint32
U8 = mybir.dt.uint8
FP8X4 = mybir.dt.float8_e4m3fn_x4
ADD = mybir.AluOpType.add
MULT = mybir.AluOpType.mult

ROWS, K, N = 4096, 1536, 768
P = 128
HB = 64
SLOTS = 12
ROW_W = SLOTS * HB
CHUNKS = (2, 2, 2, 2, 4, 4, 4, 4, 4, 4)
RING = 6
LATE = 3
RUN = 3
MOVES = ((11, 12), (4, 13), (10, 4), (2, 10), (8, 2), (0, 8), (6, 0))
REGIONS = ((1, 0), (1, 2), (1, 1), (0, 0), (0, 1), (2, 1), (2, 2))
COLS = (((0, 512),), ((0, 768),), ((256, 768),))
OPS_OF_UB = ((0, 1), (0, 1, 2), (1, 2))

FLOPS = 2 * ROWS * K * N
BYTES = ROWS * K * 2 + ROWS * N * 4 + 14 * 131072 + 10 * 131072 + N * 2


def tile_gpi_t_kernel(tc, x, w, b, mask, out):
    nc = tc.nc
    with ExitStack() as ctx:
        const = ctx.enter_context(tc.tile_pool(name="const", bufs=1))
        wpool = ctx.enter_context(tc.tile_pool(name="wpool", bufs=1))
        xpool = ctx.enter_context(tc.tile_pool(name="xpool", bufs=RING))
        oddpool = ctx.enter_context(tc.tile_pool(name="oddpool", bufs=3))
        gpool = ctx.enter_context(tc.tile_pool(name="gpool", bufs=6))
        cpool = ctx.enter_context(tc.tile_pool(name="cpool", bufs=9))
        opool = ctx.enter_context(tc.tile_pool(name="opool", bufs=8))
        ps_t = ctx.enter_context(tc.psum_pool(name="ps_t", bufs=4))
        ps_o = ctx.enter_context(tc.psum_pool(name="ps_o", bufs=4))
        ctx.enter_context(tc.manual_schedule())

        ident = const.tile([P, P], F32, name="ident")
        make_identity(nc, ident[:])
        ones = const.tile([P, P], BF16, name="ones")
        nc.vector.memset(ones[:], 1.0)
        warm = const.tile([P, 512], BF16, name="warm")
        nc.vector.memset(warm[:], 1.0)
        brow = const.tile([P, N], BF16, name="brow")
        nc.vector.memset(brow[:], 0.0)

        m_blocks = mask.rearrange("(b j e) k -> b j (e k)", b=3, j=P, e=2).rearrange(
            "b j (i k) -> b j i k", k=256
        )
        w_v = w.rearrange("(s o u p) n -> s o p u n", s=2, o=3, u=2, p=P)
        mask_sb = {}
        wt = {}

        def load_mask(ub):
            if ub == 1:
                m_t = wpool.tile([P, 2 * K], BF16, name="m1")
                nc.sync.dma_start(
                    out=m_t[:].rearrange("p (i k) -> p i k", k=256), in_=m_blocks[1]
                )
            else:
                m_t = wpool.tile([P, 4 * 256], BF16, name="m%d" % ub)
                nc.sync.dma_start(
                    out=m_t[:].rearrange("p (i k) -> p i k", k=256),
                    in_=m_blocks[ub][:, 1:12:3, :],
                )
            mask_sb[ub] = m_t

        def load_w(s, o, part=0):
            c0, c1 = COLS[o][part]
            w_t = wpool.tile([P, 2 * (c1 - c0)], BF16, name="w%d%d%d" % (s, o, part))
            nc.sync.dma_start(
                out=w_t[:].rearrange("p (u n) -> p u n", u=2), in_=w_v[s, o][:, :, c0:c1]
            )
            wt[(s, o, part)] = w_t

        def w_at(s, reg):
            o, ub = reg
            for part, (c0, c1) in enumerate(COLS[o]):
                if c0 <= 256 * ub < c1:
                    return wt[(s, o, part)], c1 - c0, 256 * ub - c0

        chunk_rows = []
        first_pair = []
        pairs = []
        r0 = 0
        for ci, jn in enumerate(CHUNKS):
            chunk_rows.append(r0)
            first_pair.append(len(pairs))
            r0 += P * jn
            for j0 in range(0, jn, 2):
                pairs.append((ci, j0))
        n_pairs = len(pairs)
        xodd = {}
        xw = {}

        def load_x(ci):
            jn = CHUNKS[ci]
            x_t = xpool.tile([P, jn * (ROW_W + 2 * HB) * 2], BF16, tag="x", name="x%d" % ci)
            ra = chunk_rows[ci]
            nc.sync.dma_start(
                out=x_t[:, 0 : jn * K].rearrange("p (j c) -> p j c", j=jn),
                in_=x[ra : ra + P * jn, :].rearrange("(p j) k -> p j k", j=jn),
            )
            xw[ci] = x_t[:].bitcast(F32)

        def row_words(ci):
            jn = CHUNKS[ci]
            return xw[ci][:, 0 : jn * ROW_W].rearrange("p (j s c) -> p j s c", j=jn, s=SLOTS)

        def move_x(ci, lo, hi):
            jn = CHUNKS[ci]
            xs = row_words(ci)
            beside = xw[ci][:, jn * ROW_W : jn * (ROW_W + 2 * HB)].rearrange(
                "p (j s c) -> p j s c", j=jn, s=2
            )
            for src, dst in MOVES[lo:hi]:
                if dst < SLOTS:
                    nc.scalar.copy(out=xs[:, :, dst, :], in_=xs[:, :, src, :])
                else:
                    nc.scalar.copy(out=beside[:, :, dst - SLOTS, :], in_=xs[:, :, src, :])

        def move_three(ci, on_vector):
            jn = CHUNKS[ci]
            odd_t = oddpool.tile([P, jn * 6 * HB], F32, tag="odd", name="odd%d" % ci)
            xs = row_words(ci)
            od = odd_t[:].rearrange("p (j s c) -> p j s c", j=jn, s=6)
            copy = nc.vector.tensor_copy if on_vector else nc.scalar.copy
            copy(out=od[:, :, 1:6:2, :], in_=xs[:, :, 0:6:2, :])
            copy(out=od[:, :, 0:6:2, :], in_=xs[:, :, 7:12:2, :])
            copy(out=xs[:, :, 0:6:2, :], in_=xs[:, :, 6:12:2, :])
            xodd[ci] = odd_t[:]

        load_mask(0)
        load_w(0, 1)
        nc.sync.dma_start(out=brow[0:1, :], in_=b.rearrange("(o n) -> o n", o=1))
        load_w(1, 1)
        load_x(0)
        load_mask(2)
        load_mask(1)
        load_w(0, 0)
        load_w(1, 0)
        load_w(0, 2)
        load_w(1, 2)
        for ci in range(1, RING):
            load_x(ci)

        def heat(bank, count):
            for k in range(count):
                nc.tensor.matmul(out=bank[:], lhsT=ones[:], rhs=warm[:], start=True, stop=True)

        pb_a = ps_o.tile([P, 512], F32, tag="O", name="pb_a")
        heat(pb_a, 5)
        nc.tensor.matmul(out=pb_a[:], lhsT=ones[:], rhs=brow[:, 0:512], start=True, stop=True)
        bias_a = const.tile([P, 512], F32, name="bias_a")
        nc.scalar.copy(out=bias_a[:], in_=pb_a[:])
        pb_b = ps_o.tile([P, 512], F32, tag="O", name="pb_b")
        for t in range(2):
            nc.tensor.matmul(
                out=pb_b[:, 256 * t : 256 * t + 256],
                lhsT=ones[:],
                rhs=brow[:, 512:768],
                start=True,
                stop=True,
            )
        bias_b = const.tile([P, 512], F32, name="bias_b")
        nc.scalar.copy(out=bias_b[:], in_=pb_b[:])

        wc = wpool.tile([P, 7 * 256], U32, name="wc", align_bytes=64)
        wsc = wpool.tile([P, 7 * 256], U8, name="wsc", align_bytes=64)
        pick = const.tile([P, 2, 192], BF16, name="pick")
        nc.gpsimd.memset(pick[:], 0.0)
        nc.gpsimd.tensor_copy(
            out=pick[:, :, 64:128], in_=ident[:].rearrange("p (m e) -> p e m", e=2)
        )
        spread = {}
        bank1 = {}
        bank2 = {}
        wtr = {}
        wgr = {}
        ORDER = ((1, 0), (0, 1), (1, 1), (0, 0))

        def t1(reg, s):
            if reg not in bank1:
                bank1[reg] = ps_o.tile([P, 512], F32, tag="O", name="t1_%d%d" % reg)
                wtr[reg] = wpool.tile([P, 1024], BF16, name="wtr%d%d" % reg)
            w_t, width, c = w_at(s, reg)
            for slot, (s_, u) in enumerate(ORDER):
                if s_ == s:
                    off = (u * width + c) // 2
                    nc.tensor.transpose(
                        bank1[reg][:, slot * P : (slot + 1) * P],
                        w_t[:].bitcast(F32)[:, off : off + P],
                        ident[:],
                    )

        def views(reg):
            bv = bank1[reg][:].bitcast(BF16).rearrange("p (l k e) -> p e l k", l=4, e=2)
            wv = wtr[reg][:].rearrange("p (e l k) -> p e l k", e=2, l=4)
            return bv, wv

        def spread_ones(reg, h, pool, tag):
            o, ub = reg
            bank = pool.tile([P, 512], F32, tag=tag, name="so%d%d_%d" % (o, ub, h))
            for u in range(2):
                for e in range(2):
                    q = 2 * u + e
                    for i, (s, us) in enumerate(ORDER[2 * u : 2 * u + 2]):
                        w_t, width, c = w_at(s, reg)
                        off = us * width + c + P * h
                        nc.tensor.matmul(
                            out=bank[:, q * P : (q + 1) * P],
                            lhsT=pick[:, e, 64 - 64 * i : 192 - 64 * i],
                            rhs=w_t[:, off : off + P],
                            start=(i == 0),
                            stop=(i == 1),
                        )
            spread[(reg, h)] = bank

        def ones_out(reg, h, on_vector=False):
            if h == 0:
                wgr[reg] = wpool.tile([P, 1024], BF16, name="wg%d%d" % reg, align_bytes=64)
            dst = wgr[reg][:, 512 * h : 512 * h + 512].rearrange("p (n q) -> p n q", q=4)
            src = spread[(reg, h)][:].rearrange("p (q n) -> p n q", q=4)
            if on_vector:
                nc.vector.tensor_copy(out=dst, in_=src)
            else:
                nc.scalar.copy(out=dst, in_=src)

        def mult(reg, s):
            o, ub = reg
            bv, wv = views(reg)
            mv = mask_sb[ub][:].rearrange("p (e h k) -> p e h k", e=2, k=P)
            f0 = 2 * o if ub == 1 else 0
            s0 = 6 + 2 * o if ub == 1 else 2
            if s == 1:
                nc.vector.tensor_tensor(
                    out=wv[:, :, 0:4:2, :], in0=bv[:, :, 0:4:2, :], in1=mv[:, :, s0 : s0 + 2, :], op=MULT
                )
            else:
                nc.vector.tensor_tensor(
                    out=wv[:, :, 1, :], in0=bv[:, :, 1, :], in1=mv[:, :, f0 + 1, :], op=MULT
                )
                nc.vector.tensor_tensor(
                    out=wv[:, :, 3, :], in0=bv[:, :, 3, :], in1=mv[:, :, f0, :], op=MULT
                )

        def t2(reg, pool, tag):
            bank2[reg] = pool.tile([P, 512], F32, tag=tag, name="t2_%d%d" % reg)
            heat(bank2[reg], 1)
            wf = wtr[reg][:].bitcast(F32)
            for i in range(4):
                nc.tensor.transpose(
                    bank2[reg][:, i * P : (i + 1) * P], wf[:, i * P : (i + 1) * P], ident[:]
                )

        def x2(reg, on_vector=False):
            wgr[reg] = wpool.tile([P, 1024], BF16, name="wg%d%d" % reg, align_bytes=64)
            dst = wgr[reg][:].bitcast(F32).rearrange("p (j e u) -> p j e u", e=2, u=2)
            src = bank2[reg][:].rearrange("p (e u j) -> p j e u", e=2, u=2)
            if on_vector:
                nc.vector.tensor_copy(out=dst, in_=src)
            else:
                nc.scalar.copy(out=dst, in_=src)

        def wq(reg):
            r = REGIONS.index(reg)
            nc.vector.quantize_mx(
                out=wc[:, r * 256 : (r + 1) * 256].bitcast(FP8X4),
                scales=wsc[:, r * 256 : (r + 1) * 256],
                in_=wgr[reg][:],
            )

        grouped = {}
        codes = {}
        ost = {}
        acc = {}

        def t_unit(k, hot=0):
            n, bk = divmod(k, 3)
            ci, j0 = pairs[n]
            pt = ps_t.tile([P, 512], F32, tag="T", name="pt%d_%d" % (n, bk))
            heat(pt, hot)
            for sl in range(2):
                t, o = divmod(2 * bk + sl, 3)
                for u in range(2):
                    if u == 1 and ci in xodd:
                        off = (j0 + t) * 6 * HB + HB * 2 * o
                        words = xodd[ci][:, off : off + P]
                    else:
                        off = (j0 + t) * ROW_W + HB * (2 * o + 7 * u)
                        if (o, u) == (2, 1):
                            off = CHUNKS[ci] * ROW_W + (j0 + t) * 2 * HB
                        words = xw[ci][:, off : off + P]
                    i = 2 * sl + u
                    nc.tensor.transpose(pt[:, i * P : (i + 1) * P], words, ident[:])
            grp = gpool.tile([P, 1024], BF16, tag="g", name="g%d_%d" % (n, bk), align_bytes=64)
            nc.scalar.copy(
                out=grp[:].bitcast(F32).rearrange("p (s r u) -> p s r u", s=2, u=2),
                in_=pt[:].rearrange("p (s u r) -> p s r u", s=2, u=2),
            )
            grouped[k] = grp
            for c2 in range(4, len(CHUNKS)):
                i = k - 3 * first_pair[c2] + 7
                if 0 <= i < 6:
                    move_x(c2, i + min(i, 1), i + 2)
            if bk == 2 and j0 + 2 == CHUNKS[ci] and ci + RING < len(CHUNKS):
                load_x(ci + RING)

        def quant(k):
            cod = cpool.tile([P, 256], U32, tag="c", name="c%d" % k, align_bytes=64)
            scl = cpool.tile([P, 256], U8, tag="s", name="s%d" % k, align_bytes=64)
            nc.vector.quantize_mx(out=cod[:].bitcast(FP8X4), scales=scl[:], in_=grouped[k][:])
            codes[k] = (cod, scl)

        def one_pass(n, t, ub, o, dst):
            ops = OPS_OF_UB[ub]
            if (n, ub) == (0, 1):
                ops = (1, 0, 2)
            bk, sl = divmod(3 * t + o, 2)
            cod, scl = codes[3 * n + bk]
            r = REGIONS.index((o, ub))
            nc.tensor.matmul_mx(
                out=dst,
                lhsT=cod[:, sl * P : (sl + 1) * P].bitcast(FP8X4),
                lhsT_scale=scl[:, sl * P : (sl + 1) * P],
                rhs=wc[:, r * 256 : (r + 1) * 256].bitcast(FP8X4),
                rhs_scale=wsc[:, r * 256 : (r + 1) * 256],
                start=(o == ops[0]),
                stop=(o == ops[-1]),
            )

        def acc_part(n, t, ub):
            if ub == 2:
                return acc[(n, 2)][:, 256 * t : 256 * t + 256]
            return acc[(n, t)][:, 256 * ub : 256 * ub + 256]

        def new_acc(n, i):
            acc[(n, i)] = ps_o.tile([P, 512], F32, tag="O", name="acc%d_%d" % (n, i))

        def mx_first(part):
            if part == 0:
                for i in range(3):
                    new_acc(0, i)
                order = [(t, 0, o) for t in range(2) for o in range(2)]
            elif part == 1:
                order = [(t, 1, o) for t in range(2) for o in (1, 0)]
            else:
                order = [(0, 1, 2), (1, 1, 2)]
                order += [(t, 2, o) for t in range(2) for o in (1, 2)]
            for t, ub, o in order:
                one_pass(0, t, ub, o, acc_part(0, t, ub))

        def mx_unit(k):
            n, i = divmod(k, 3)
            new_acc(n, i)
            for t, ub in (((0, 2), (1, 2)) if i == 2 else ((i, 0), (i, 1))):
                for o in OPS_OF_UB[ub]:
                    one_pass(n, t, ub, o, acc_part(n, t, ub))

        def out_rows(n):
            ci, j0 = pairs[n]
            jn = CHUNKS[ci]
            ra = chunk_rows[ci]
            dst = out[ra : ra + P * jn, :].rearrange("(p j) n -> p j n", j=jn)
            return dst[:, j0 : j0 + 2, :]

        def evac(k):
            n, i = divmod(k, 3)
            if n not in ost:
                ost[n] = opool.tile([P, 2 * N], F32, tag="o", name="o%d" % n)
            ov = ost[n][:].rearrange("p (j n) -> p j n", n=N)
            late = n >= n_pairs - LATE
            dst = out_rows(n)
            if i < 2:
                nc.vector.tensor_tensor(
                    out=ov[:, i, 0:512], in0=acc[(n, i)][:], in1=bias_a[:], op=ADD
                )
                if late:
                    nc.sync.dma_start(out=dst[:, i, 0:512], in_=ov[:, i, 0:512])
            else:
                nc.vector.tensor_tensor(
                    out=ov[:, :, 512:768],
                    in0=acc[(n, 2)][:].rearrange("p (t n) -> p t n", t=2),
                    in1=bias_b[:].rearrange("p (t n) -> p t n", t=2),
                    op=ADD,
                )
                if late:
                    nc.sync.dma_start(out=dst[:, :, 512:768], in_=ov[:, :, 512:768])
                else:
                    nc.sync.dma_start(out=dst, in_=ov)

        def last_pair():
            n = n_pairs - 1
            dst = out_rows(n)
            ost[n] = opool.tile([P, 2 * N], F32, tag="o", name="o%d" % n)
            ov = ost[n][:].rearrange("p (j n) -> p j n", n=N)
            mx_unit(3 * n + 2)
            evac(3 * n + 2)
            mx_unit(3 * n)
            evac(3 * n)
            for ub in (1, 0):
                part = ps_t.tile([P, 512], F32, tag="T", name="end%d" % ub)
                cols = slice(256 * ub, 256 * ub + 256)
                for o in OPS_OF_UB[ub]:
                    one_pass(n, 1, ub, o, part[:, 0:256])
                nc.vector.tensor_tensor(
                    out=ov[:, 1, cols], in0=part[:, 0:256], in1=bias_a[:, cols], op=ADD
                )
                nc.sync.dma_start(out=dst[:, 1, cols], in_=ov[:, 1, cols])

        b0, b2, b1, a0, a1, c1r, c2r = REGIONS
        t1(b0, 0)
        t1(b0, 1)
        t1(b2, 0)
        t1(b2, 1)
        t1(b1, 0)
        t1(b1, 1)
        mult(b0, 1)
        mult(b0, 0)
        t2(b0, ps_t, "T")
        move_three(0, True)
        x2(b0)
        for k in range(3):
            t_unit(k, 1)
        mult(b2, 1)
        mult(b2, 0)
        wq(b0)
        quant(0)
        t2(b2, ps_t, "T")
        x2(b2)
        mult(b1, 1)
        mult(b1, 0)
        quant(1)
        quant(2)
        wq(b2)
        spread_ones(a0, 0, ps_o, "O")
        spread_ones(a0, 1, ps_o, "O")
        t1(a1, 0)
        t1(a1, 1)
        t2(b1, ps_t, "T")
        ones_out(a0, 0)
        ones_out(a0, 1)
        x2(b1)
        mult(a1, 1)
        mult(a1, 0)
        wq(b1)
        spread_ones(c2r, 0, ps_o, "O")
        spread_ones(c2r, 1, ps_o, "O")
        t1(c1r, 0)
        t1(c1r, 1)
        t2(a1, ps_t, "T")
        ones_out(c2r, 0)
        ones_out(c2r, 1)
        wq(a0)
        mult(c1r, 1)
        mult(c1r, 0)
        mx_first(0)
        x2(a1)
        wq(a1)
        t2(c1r, ps_t, "T")
        x2(c1r)
        move_three(1, True)
        wq(c2r)
        wq(c1r)
        move_three(2, True)
        move_three(3, True)

        n_units = 3 * n_pairs
        mx_first(1)
        for k in range(3, 6):
            t_unit(k, 0)
            quant(k)
        mx_first(2)
        evac(0)
        evac(1)
        evac(2)
        for k in range(6, 6 + RUN):
            t_unit(k)
        done_t = 6 + RUN
        done_q = 6
        for k0 in range(3, n_units - 3, RUN):
            ks = range(k0, min(k0 + RUN, n_units - 3))
            if done_q < done_t:
                quant(done_q)
                done_q += 1
            for k in ks:
                mx_unit(k)
                if done_q < done_t:
                    quant(done_q)
                    done_q += 1
                evac(k)
            for k in range(done_t, min(done_t + RUN, n_units)):
                t_unit(k)
            done_t = min(done_t + RUN, n_units)
        last_pair()
